import numpy as np
import ml_dtypes


def mxq(x, axis, fmt="e4m3"):
    dtype, down = {"e4m3": (ml_dtypes.float8_e4m3fn, 7), "e5m2": (ml_dtypes.float8_e5m2, 14)}[fmt]
    v = np.moveaxis(np.asarray(x, np.float32).astype(ml_dtypes.bfloat16).astype(np.float64), axis, -1)
    blocks = v.reshape(v.shape[:-1] + (-1, 32))
    amax = np.abs(blocks).max(-1, keepdims=True)
    byte = np.maximum(np.where(amax > 0, np.frexp(amax)[1] - 1 + 127, 0) - down, 1)
    scale = np.exp2(byte - 127.0)
    codes = (blocks / scale).astype(np.float32).astype(dtype).astype(np.float64)
    return np.moveaxis((codes * scale).reshape(v.shape), -1, axis)


WIDE = False


def mx_kscale(k):
    if not WIDE:
        return np.ones(k)
    levels = np.array([10, -10, 5, -5, 0])
    if k % 512:
        return np.exp2(np.random.permutation(np.resize(levels, k // 32))).repeat(32)
    a = np.empty((k // 512, 16))
    for p in range(k // 512):
        a[p, :8] = np.random.permutation(np.resize(levels, 8))
        for g in range(8):
            far = levels[np.abs(levels - a[p, g]) >= 10]
            a[p, g + 8] = far[np.random.randint(len(far))]
    return np.exp2(a.ravel()).repeat(32)


BF16 = ml_dtypes.bfloat16


def bf(x):
    return np.asarray(x, np.float32).astype(BF16)


def f64(x):
    return np.asarray(x).astype(np.float64)


E2M1 = np.array([0.0, 0.5, 1.0, 1.5, 2.0, 3.0, 4.0, 6.0, -0.0, -0.5, -1.0, -1.5, -2.0, -3.0, -4.0, -6.0])


def pack_weight(w, fmt):
    k, n = w.shape
    w = f64(bf(w)).reshape(k // 32, 32, n)
    amax = np.abs(w).max(1)
    if fmt == "e4m3":
        byte = np.frexp(amax)[1] - 1 + 127 - 7
    else:
        mant, ex = np.frexp(amax / 6.0)
        byte = np.where(mant > 0.5, ex, ex - 1) + 127
    byte = np.clip(np.where(amax > 0, byte, 1), 1, 254)
    scaled = (w * np.exp2(127.0 - byte)[:, None, :]).reshape(k, n).astype(np.float32)
    by_word = np.ascontiguousarray(scaled.reshape(k // 512, 128, 4, n).transpose(0, 1, 3, 2))
    if fmt == "e4m3":
        words = by_word.astype(ml_dtypes.float8_e4m3fn).view(np.uint8)
    else:
        c = by_word.astype(ml_dtypes.float4_e2m1fn).view(np.uint8) & 0xF
        words = c[..., 0::2] | (c[..., 1::2] << 4)
    return np.ascontiguousarray(words), np.ascontiguousarray(byte.astype(np.uint8).reshape(k // 512, 16, n))


def unpack_weight(words, scales, fmt):
    g, p, n, _ = words.shape
    if fmt == "e4m3":
        vals = np.ascontiguousarray(words).view(ml_dtypes.float8_e4m3fn).astype(np.float64)
    else:
        nib = np.empty((g, p, n, 4), np.uint8)
        nib[..., 0::2] = words & 0xF
        nib[..., 1::2] = words >> 4
        vals = E2M1[nib]
    vals = vals * np.repeat(np.exp2(scales.astype(np.float64) - 127.0), 8, axis=1)[..., None]
    return vals.transpose(0, 1, 3, 2).reshape(g * 512, n)


B, N, ATTR, STATE, REL, G, NF = 4, 32, 4, 16, 9, 32, 1024


def draw0():
    rn = np.random.standard_normal
    s, u, t = mx_kscale(NF), mx_kscale(NF), mx_kscale(NF)
    rp_rows = np.concatenate([s, u, u])
    pp_rows = np.concatenate([u, t])
    pp_scale = np.concatenate([np.full(NF, 1.0 / np.sqrt(NF)), np.full(NF, 1.0 / np.sqrt(NF * N))])
    rel_enc = bf(np.maximum(rn((B, N, N, NF)) * 1.1, 0.0) * s)
    obj = bf(np.maximum(rn((B, N, NF)) * 1.1, 0.0) * u)
    rp_w_words, rp_w_scales = pack_weight(rn((3 * NF, NF)) * 2.0 / np.sqrt(3 * NF * N) / rp_rows[:, None] * t, "e4m3")
    rp_b = bf(rn(NF) * 0.1 * t)
    pp_w_words, pp_w_scales = pack_weight(rn((2 * NF, NF)) * (pp_scale / pp_rows)[:, None], "e4m3")
    pp_b = bf(rn(NF) * 0.1)
    return {
        "rel_enc": rel_enc,
        "obj": obj,
        "rp_w_words": rp_w_words,
        "rp_w_scales": rp_w_scales,
        "rp_b": rp_b,
        "pp_w_words": pp_w_words,
        "pp_w_scales": pp_w_scales,
        "pp_b": pp_b,
    }


def core(rel_enc, obj, rp_w_words, rp_w_scales, rp_b, pp_w_words, pp_w_scales, pp_b):
    rp, pp = unpack_weight(rp_w_words, rp_w_scales, "e4m3"), unpack_weight(pp_w_words, pp_w_scales, "e4m3")
    oq = mxq(f64(obj), 2, "e4m3")
    e_rel = mxq(f64(rel_enc), 3, "e4m3") @ rp[:NF]
    e_recv = oq @ rp[NF:2 * NF]
    e_send = oq @ rp[2 * NF:]
    rel_eff = np.maximum(e_rel + e_recv[:, :, None, :] + e_send[:, None, :, :] + f64(rp_b), 0.0)
    agg = rel_eff.sum(axis=2)
    p_obj = oq @ pp[:NF]
    p_agg = mxq(agg, 2, "e4m3") @ pp[NF:]
    return np.maximum(p_obj + p_agg + f64(pp_b), 0.0)


def e4m3fn_bytes(y):
    return np.clip(np.asarray(y, np.float64), -448.0, 448.0).astype(np.float32).astype(ml_dtypes.float8_e4m3fn).view(np.uint8)


def e4m3fn_values(b):
    return np.asarray(b, np.uint8).view(ml_dtypes.float8_e4m3fn).astype(np.float64)


def setup_inputs():
    d = draw0()
    x0 = np.asarray(d['rel_enc']).astype(np.float64)
    s = (np.max(np.abs(x0), axis=(0, 1, 2), keepdims=True) / 448.0).astype(np.float32)
    out = {}
    for k, v in d.items():
        if k == 'rel_enc':
            out['rel_enc_bytes'] = e4m3fn_bytes(x0 / s.astype(np.float64))
            out['rel_enc_scale'] = s
        else:
            out[k] = v
    return out


def reference(rel_enc_bytes, rel_enc_scale, obj, rp_w_words, rp_w_scales, rp_b, pp_w_words, pp_w_scales, pp_b):
    return core(e4m3fn_values(rel_enc_bytes) * rel_enc_scale.astype(np.float64), obj, rp_w_words, rp_w_scales, rp_b, pp_w_words, pp_w_scales, pp_b)

@@ -1,0 +1,466 @@
+from contextlib import ExitStack
+
+import concourse.mybir as mybir
+from concourse.masks import make_identity
+
+F32 = mybir.dt.float32
+BF16 = mybir.dt.bfloat16
+I32 = mybir.dt.int32
+U32 = mybir.dt.uint32
+U8 = mybir.dt.uint8
+FP8 = mybir.dt.float8_e4m3fn
+FP8X4 = mybir.dt.float8_e4m3fn_x4
+ALU = mybir.AluOpType
+ACT = mybir.ActivationFunctionType
+AX = mybir.AxisListType
+
+P = 128
+B, N, NF = 4, 32, 1024
+GROUPS = 2
+M_TILES = 8
+CHUNKS = 8
+FLOPS = 2 * 4096 * NF * NF + 4 * 2 * 128 * NF * NF
+
+HALVES = (((2, "a"), (0, "g"), (1, "b"), (3, "g")), ((5, "a"), (4, "b"), (6, "g"), (7, "b")))
+LAST = (((2, "a"), (0, "g"), (1, "v"), (3, "g")), ((5, "g"), (4, "v"), (6, "b"), (7, "b")))
+
+
+def tile_compositionalkoopmanoperators_pa_w8_kernel(
+    tc, rel_enc_bytes, rel_enc_scale, obj, rp_w_words, rp_w_scales, rp_b, pp_w_words, pp_w_scales, pp_b, out
+):
+    nc = tc.nc
+    with ExitStack() as ctx:
+        keep = ctx.enter_context(tc.tile_pool(name="keep", bufs=1))
+        stream = ctx.enter_context(tc.tile_pool(name="stream", bufs=2))
+        psum = ctx.enter_context(tc.psum_pool(name="psum", bufs=1))
+
+        rel_rows = rel_enc_bytes.rearrange("b i j k -> (b i j) k")
+        out_rows = out.rearrange("b i n -> (b i) n")
+        rp_words = rp_w_words.rearrange("g p n t -> p g (n t)").bitcast(I32)
+        pp_words = pp_w_words.rearrange("g p n t -> p g (n t)").bitcast(I32)
+
+        ident = keep.tile([P, P], F32, name="ident")
+        make_identity(nc, ident[:])
+
+        scale_sb = keep.tile([P, GROUPS, 4], F32, name="scale_sb")
+        bias_row = keep.tile([P, P], BF16, name="bias_row")
+        bias_rowf = keep.tile([P, P], F32, name="bias_rowf")
+        bias_col = keep.tile([P, M_TILES], F32, name="bias_col")
+        ppb = keep.tile([P, NF], BF16, name="ppb")
+        obj_sb = keep.tile([P, NF], BF16, name="obj_sb")
+        obj_grp = keep.tile([P, GROUPS * 512], BF16, name="obj_grp", align_bytes=64)
+        obj_codes = keep.tile([P, GROUPS * P], U32, name="obj_codes", align_bytes=64)
+        obj_sc = keep.tile([P, GROUPS * P], U8, name="obj_sc", align_bytes=64)
+        srep_codes = keep.tile([P, B, GROUPS, 512], U32, name="srep_codes", align_bytes=64)
+        srep_sc = keep.tile([P, B, GROUPS, 512], U8, name="srep_sc", align_bytes=64)
+        w_rel = [keep.tile([P, 2, 512], U32, name="w_rel%d" % h, align_bytes=64) for h in range(2)]
+        w_obj = [keep.tile([P, 4, 512], U32, name="w_obj%d" % h, align_bytes=64) for h in range(2)]
+        w_pp = keep.tile([P, 4, NF], U32, name="w_pp", align_bytes=64)
+        pl_a = keep.tile([P, NF], U8, name="pl_a", align_bytes=64)
+        pl_b = keep.tile([P, NF], U8, name="pl_b", align_bytes=64)
+        pl_c = keep.tile([P, NF], U8, name="pl_c", align_bytes=64)
+        recv = keep.tile([P, M_TILES, P], F32, name="recv")
+        neg_recv = keep.tile([P, M_TILES, P], F32, name="neg_recv")
+        split = keep.tile([P, M_TILES, P], F32, name="split")
+        send = keep.tile([P, M_TILES, P], F32, name="send")
+        agg = keep.tile([P, M_TILES, P], F32, name="agg")
+        agg_bf = keep.tile([P, 2, 512], BF16, name="agg_bf")
+        agg_grp = keep.tile([P, 2, 512], BF16, name="agg_grp", align_bytes=64)
+        agg_codes = keep.tile([P, 2, P], U32, name="agg_codes", align_bytes=64)
+        agg_sc = keep.tile([P, 2, P], U8, name="agg_sc", align_bytes=64)
+        warm = keep.tile([P, 1], F32, name="warm")
+
+        def w_codes(g, m):
+            lo = (m % 4) * P
+            tile = w_rel[m // 4][:, g, lo : lo + P] if g < 2 else w_obj[m // 4][:, g - 2, lo : lo + P]
+            return tile.bitcast(FP8X4)
+
+        def w_scale(g, m):
+            plane = pl_a if g < 4 else pl_b
+            return plane[4 * (g % 4) : P, m * P : m * P + P]
+
+        raw, wide, xbank, grp, codes, scales, banks, sums = {}, {}, {}, {}, {}, {}, {}, {}
+        pending = {m: [] for m in range(M_TILES)}
+
+        def e_bank():
+            bank = psum.tile([P, 512], F32, name="e_bank", tag="e", bufs=6)
+            return bank
+
+        def load(p):
+            t = stream.tile([P, 2, NF], U8, name="rel_bytes", tag="rel_bytes", bufs=6)
+            src = rel_rows[256 * p : 256 * p + 256, :].rearrange("(s q) k -> q s k", q=P)
+            if p == 0:
+                for s in range(2):
+                    nc.sync.dma_start(out=t[:, s, :], in_=src[:, s, :])
+            else:
+                nc.sync.dma_start(out=t[:], in_=src)
+            raw[p] = t
+
+        def widen(p):
+            t = stream.tile([P, 2, NF], BF16, name="rel_wide", tag="rel_wide", bufs=3)
+            if p == 0:
+                for s in range(2):
+                    nc.scalar.copy(out=t[:, s, :], in_=raw[p][:, s, :].bitcast(FP8))
+            else:
+                nc.scalar.copy(
+                    out=t[:].rearrange("p s k -> p (s k)"),
+                    in_=raw[p][:].rearrange("p s k -> p (s k)").bitcast(FP8),
+                )
+            wide[p] = t
+
+        def turn(p):
+            words = wide[p][:].bitcast(F32)
+            for g in range(GROUPS):
+                bank = psum.tile([P, 2, 256], F32, name="x%d" % g, tag="x%d" % g, bufs=1)
+                for s in range(2):
+                    for u in range(2):
+                        nc.tensor.transpose(
+                            bank[:, u, P * s : P * s + P], words[:, s, 256 * g + u : 256 * g + 256 : 2], ident[:]
+                        )
+                xbank[p, g] = bank
+
+        def scale_mul(p, g):
+            t = stream.tile([P, 256, 4], BF16, name="grp%d" % g, tag="grp%d" % g, bufs=2, align_bytes=64)
+            src = xbank[p, g][:].rearrange("p u c -> p (u c)").bitcast(BF16)
+            nc.vector.tensor_tensor(
+                out=t[:].rearrange("p c (u e) -> p c u e", u=2),
+                in0=src.rearrange("p (u c e) -> p c u e", u=2, e=2),
+                in1=scale_sb[:, g, :].rearrange("p (o u e) -> p o u e", o=1, u=2).to_broadcast([P, 256, 2, 2]),
+                op=ALU.mult,
+            )
+            grp[p, g] = t
+
+        def quant(p, g):
+            c, h = p // 2, p % 2
+            if c not in codes:
+                ct = stream.tile([P, GROUPS, 512], U32, name="codes", tag="codes", bufs=3, align_bytes=64)
+                st = stream.tile([P, GROUPS, 512], U8, name="scales", tag="scales", bufs=3, align_bytes=64)
+                codes[c], scales[c] = ct, st
+            cols = slice(256 * h, 256 * h + 256)
+            nc.vector.quantize_mx(
+                out=codes[c][:, g, cols].bitcast(FP8X4),
+                scales=scales[c][:, g, cols],
+                in_=grp[p, g][:].rearrange("p c t -> p (c t)"),
+            )
+
+        def replicate(b):
+            oc = obj_codes[:].bitcast(I32).rearrange("p (g o t) -> p g o t", g=GROUPS, o=1)
+            osc = obj_sc[:].bitcast(I32).rearrange("p (g o t) -> p g o t", g=GROUPS, o=1)
+            nc.vector.tensor_copy(
+                out=srep_codes[:, b].rearrange("p g (r j) -> p g r j", r=16).bitcast(I32),
+                in_=oc[:, :, :, 32 * b : 32 * b + 32].to_broadcast([P, GROUPS, 16, 32]),
+            )
+            nc.vector.tensor_copy(
+                out=srep_sc[:, b].rearrange("p g (r j) -> p g r j", r=16).bitcast(I32),
+                in_=osc[:, :, :, 8 * b : 8 * b + 8].to_broadcast([P, GROUPS, 16, 8]),
+            )
+
+        def products(c, m, mode):
+            b = c // 2
+            bank = e_bank()
+            passes = []
+            if mode in "ab":
+                for g in range(GROUPS):
+                    passes.append((4 + g, srep_codes[:, b, g, :], srep_sc[:, b, g, :]))
+            for g in range(GROUPS):
+                passes.append((g, codes[c][:, g, :], scales[c][:, g, :]))
+            for k, (g, mc, ms) in enumerate(passes):
+                nc.tensor.matmul_mx(
+                    out=bank[:],
+                    lhsT=w_codes(g, m),
+                    lhsT_scale=w_scale(g, m),
+                    rhs=mc.bitcast(FP8X4),
+                    rhs_scale=ms,
+                    start=(k == 0),
+                    stop=(k == len(passes) - 1),
+                )
+            banks[c, m] = bank
+
+        def cols_of(c):
+            lo = 32 * (c // 2) + 16 * (c % 2)
+            return slice(lo, lo + 16)
+
+        def add_send(c, m):
+            b = c // 2
+            t = stream.tile([P, 16, 32], F32, name="sum_t", tag="sum_t", bufs=4)
+            nc.vector.tensor_tensor(
+                out=t[:],
+                in0=banks[c, m][:].rearrange("p (i j) -> p i j", i=16),
+                in1=send[:, m : m + 1, 32 * b : 32 * b + 32].to_broadcast([P, 16, 32]),
+                op=ALU.add,
+            )
+            sums[c, m] = t
+
+        def clip(c, m, mode):
+            src = banks[c, m][:].rearrange("p (i j) -> p i j", i=16) if mode == "b" else sums[c, m][:]
+            t = stream.tile([P, 16, 32], F32, name="clip_t", tag="clip_t", bufs=3)
+            nc.vector.tensor_tensor(
+                out=t[:],
+                in0=src,
+                in1=neg_recv[:, m, cols_of(c)].unsqueeze(2).to_broadcast([P, 16, 32]),
+                op=ALU.max,
+            )
+            sums[c, m] = t
+
+        def reduce_j(c, m):
+            nc.vector.tensor_reduce(out=agg[:, m, cols_of(c)], in_=sums[c, m][:], axis=AX.X, op=ALU.add)
+            pending[m].append(cols_of(c))
+
+        def undo(c, m):
+            if c % 2 == 1 and pending[m]:
+                cols = slice(pending[m][0].start, pending[m][-1].stop)
+                nc.vector.scalar_tensor_tensor(
+                    out=agg[:, m, cols],
+                    in0=neg_recv[:, m, cols],
+                    scalar=-32.0,
+                    in1=agg[:, m, cols],
+                    op0=ALU.mult,
+                    op1=ALU.add,
+                )
+                pending[m].clear()
+
+        def relu_sum(c, m, mode):
+            src = banks[c, m][:] if mode == "a" else sums[c, m][:].rearrange("p i j -> p (i j)")
+            junk = stream.tile([P, 512], BF16, name="junk", tag="junk", bufs=3)
+            lo = cols_of(c).start
+            for i in range(16):
+                nc.scalar.activation(
+                    out=junk[:, 32 * i : 32 * i + 32],
+                    in_=src[:, 32 * i : 32 * i + 32],
+                    func=ACT.Relu,
+                    bias=recv[:, m, lo + i : lo + i + 1],
+                    accum_out=agg[:, m, lo + i : lo + i + 1],
+                )
+
+        def obj_products(group, hf):
+            bank = e_bank()
+            for k in range(4):
+                for g in range(GROUPS):
+                    nc.tensor.matmul_mx(
+                        out=bank[:, P * k : P * k + P],
+                        lhsT=w_codes(group + g, 4 * hf + k),
+                        lhsT_scale=w_scale(group + g, 4 * hf + k),
+                        rhs=obj_codes[:, P * g : P * g + P].bitcast(FP8X4),
+                        rhs_scale=obj_sc[:, P * g : P * g + P],
+                        start=(g == 0),
+                        stop=(g == 1),
+                    )
+            return bank
+
+        def merge(a, b):
+            res = []
+            for k in range(max(len(a), len(b))):
+                if k < len(a):
+                    res.append(a[k])
+                if k < len(b):
+                    res.append(b[k])
+            return res
+
+        def slot(s, tiles):
+            c = s // 2
+            prep = s + 2 < 16
+            for m, mode in tiles[:2]:
+                products(c, m, mode)
+            lanes = {"a": [], "g": [("A",)], "b": [("B",), ("C",)], "v": [("A",), ("B",), ("C",)]}
+            per = [[(op[0], m, mode) for op in lanes[mode]] for m, mode in tiles]
+            per = [x for x in per if x]
+            depth = max(len(x) for x in per)
+            order = []
+            for k in range(depth):
+                for x in per:
+                    if k < len(x):
+                        order.append(x[k])
+            pv = [("M", 0), ("M", 1), ("Q", 0), ("Q", 1)] if prep else []
+            emitted = [m for m, mode in tiles[:2]]
+
+            def rest():
+                if s + 3 < 16:
+                    turn(s + 3)
+                for m, mode in tiles[2:]:
+                    products(c, m, mode)
+
+            for item in merge(pv, order):
+                if item[0] == "M":
+                    scale_mul(s + 2, item[1])
+                    continue
+                if item[0] == "Q":
+                    quant(s + 2, item[1])
+                    continue
+                if item[1] not in emitted:
+                    rest()
+                    emitted.extend([m for m, mode in tiles])
+                if item[0] == "A":
+                    add_send(c, item[1])
+                elif item[0] == "B":
+                    clip(c, item[1], item[2])
+                else:
+                    reduce_j(c, item[1])
+                    undo(c, item[1])
+            first = True
+            for m, mode in tiles:
+                if mode in "ag":
+                    relu_sum(c, m, mode)
+                    if first and s + 4 < 16:
+                        widen(s + 4)
+                    first = False
+
+        with tc.manual_schedule():
+            load(0)
+            nc.sync.dma_start(
+                out=scale_sb[:], in_=rel_enc_scale.rearrange("a b c (g p t) -> p (a b c g) t", p=P, t=4)
+            )
+            nc.sync.dma_start(out=obj_sb[:], in_=obj.rearrange("b i k -> (b i) k"))
+            load(1)
+            for plane in (pl_a, pl_b, pl_c):
+                nc.vector.memset(plane[:].bitcast(I32), 0)
+            nc.vector.memset(obj_sc[:].bitcast(I32), 0)
+            nc.vector.memset(bias_row[:], 0.0)
+            nc.vector.memset(warm[:], 0.0)
+            nc.scalar.activation(out=warm[:], in_=warm[:], func=ACT.Relu)
+            for q in range(4):
+                nc.sync.dma_start(
+                    out=pl_a[32 * q : 32 * q + 16, :].bitcast(I32),
+                    in_=rp_w_scales[0:4, 4 * q : 4 * q + 4, :].bitcast(I32),
+                )
+            for q in range(4):
+                nc.sync.dma_start(
+                    out=pl_b[32 * q : 32 * q + 8, :].bitcast(I32),
+                    in_=rp_w_scales[4:6, 4 * q : 4 * q + 4, :].bitcast(I32),
+                )
+            nc.sync.dma_start(out=w_obj[0][:].bitcast(I32), in_=rp_words[:, 2:6, 0:512])
+            nc.sync.dma_start(out=w_rel[0][:].bitcast(I32), in_=rp_words[:, 0:2, 0:512])
+            nc.sync.dma_start(out=bias_row[0:M_TILES, :], in_=rp_b.rearrange("(m p) -> m p", p=P))
+            load(2)
+            nc.sync.dma_start(out=w_obj[1][:].bitcast(I32), in_=rp_words[:, 2:6, 512:1024])
+            nc.sync.dma_start(out=w_rel[1][:].bitcast(I32), in_=rp_words[:, 0:2, 512:1024])
+            load(3)
+            load(4)
+
+            widen(0)
+            turn(0)
+            obj_bank = e_bank()
+            obj_words = obj_sb[:].bitcast(F32)
+            for g in range(GROUPS):
+                for u in range(2):
+                    k = 2 * g + u
+                    nc.tensor.transpose(
+                        obj_bank[:, P * k : P * k + P], obj_words[:, 256 * g + u : 256 * g + 256 : 2], ident[:]
+                    )
+            widen(1)
+            nc.scalar.copy(
+                out=obj_grp[:].bitcast(F32).rearrange("p (g c u) -> p g c u", g=GROUPS, u=2),
+                in_=obj_bank[:].rearrange("p (g u c) -> p g c u", g=GROUPS, u=2),
+            )
+            scale_mul(0, 0)
+            scale_mul(0, 1)
+            nc.vector.quantize_mx(out=obj_codes[:].bitcast(FP8X4), scales=obj_sc[:], in_=obj_grp[:])
+            quant(0, 0)
+            quant(0, 1)
+            turn(1)
+            replicate(0)
+            scale_mul(1, 0)
+            scale_mul(1, 1)
+            nc.vector.tensor_copy(out=bias_rowf[:], in_=bias_row[:])
+            quant(1, 0)
+            quant(1, 1)
+            bias_bank = e_bank()
+            nc.tensor.transpose(bias_bank[:, 0:P], bias_rowf[:], ident[:])
+            nc.scalar.copy(out=bias_col[:], in_=bias_bank[:, 0:M_TILES])
+
+            def receivers(hf):
+                bank = obj_products(2, hf)
+                for k in range(4):
+                    m = 4 * hf + k
+                    nc.scalar.activation(
+                        out=recv[:, m, :],
+                        in_=bank[:, P * k : P * k + P],
+                        func=ACT.Identity,
+                        bias=bias_col[:, m : m + 1],
+                    )
+
+            def senders(hf):
+                bank = obj_products(4, hf)
+                nc.vector.tensor_copy(
+                    out=send[:, 4 * hf : 4 * hf + 4, :].rearrange("p m c -> p (m c)"), in_=bank[:]
+                )
+
+            def negate(hf):
+                ms = slice(4 * hf, 4 * hf + 4)
+                nc.vector.scalar_tensor_tensor(
+                    out=split[:, ms, :], in0=recv[:, ms, :], scalar=33.0, in1=recv[:, ms, :],
+                    op0=ALU.mult, op1=ALU.subtract,
+                )
+                nc.vector.scalar_tensor_tensor(
+                    out=neg_recv[:, ms, :], in0=recv[:, ms, :], scalar=-33.0, in1=split[:, ms, :],
+                    op0=ALU.mult, op1=ALU.add,
+                )
+
+            receivers(0)
+            senders(0)
+            widen(2)
+            turn(2)
+            negate(0)
+            widen(3)
+            receivers(1)
+            senders(1)
+            negate(1)
+
+            for s in range(16):
+                if s + 5 < 16:
+                    load(s + 5)
+                if s == 1:
+                    for q in range(4):
+                        nc.sync.dma_start(
+                            out=pl_c[32 * q : 32 * q + 16, :].bitcast(I32),
+                            in_=pp_w_scales[:, 4 * q : 4 * q + 4, :].bitcast(I32),
+                        )
+                if s in (2, 4, 6, 8):
+                    g = s // 2 - 1
+                    nc.sync.dma_start(out=w_pp[:, g, :].bitcast(I32), in_=pp_words[:, g, :])
+                if s == 9:
+                    nc.sync.dma_start(out=ppb[:], in_=pp_b.partition_broadcast(P))
+                if s % 4 == 2 and s < 12:
+                    replicate(s // 4 + 1)
+                slot(s, (LAST if s >= 14 else HALVES)[s % 2])
+
+            out_banks = [e_bank(), e_bank()]
+
+            def out_pass(act_codes, act_scales, g, first, last):
+                for n in range(2):
+                    nc.tensor.matmul_mx(
+                        out=out_banks[n][:],
+                        lhsT=act_codes.bitcast(FP8X4),
+                        lhsT_scale=act_scales,
+                        rhs=w_pp[:, g, 512 * n : 512 * n + 512].bitcast(FP8X4),
+                        rhs_scale=pl_c[4 * g : P, 512 * n : 512 * n + 512],
+                        start=first,
+                        stop=last,
+                    )
+
+            for g in range(GROUPS):
+                out_pass(obj_codes[:, P * g : P * g + P], obj_sc[:, P * g : P * g + P], g, g == 0, False)
+            for hf in range(2):
+                rows = e_bank()
+                for k in range(4):
+                    nc.tensor.transpose(rows[:, P * k : P * k + P], agg[:, 4 * hf + k, :], ident[:])
+                nc.vector.tensor_copy(out=agg_bf[:, hf, :], in_=rows[:])
+                agg_words = agg_bf[:, hf, :].bitcast(F32)
+                back = e_bank()
+                for u in range(2):
+                    nc.tensor.transpose(back[:, P * u : P * u + P], agg_words[:, u:256:2], ident[:])
+                nc.vector.tensor_copy(
+                    out=agg_grp[:, hf, :].bitcast(F32).rearrange("p (c u) -> p c u", u=2),
+                    in_=back[:, 0:256].rearrange("p (u c) -> p c u", u=2),
+                )
+                nc.vector.quantize_mx(
+                    out=agg_codes[:, hf, :].bitcast(FP8X4), scales=agg_sc[:, hf, :], in_=agg_grp[:, hf, :]
+                )
+                out_pass(agg_codes[:, hf, :], agg_sc[:, hf, :], 2 + hf, False, hf == 1)
+            for n in range(2):
+                res = stream.tile([P, 512], F32, name="res", tag="res", bufs=2)
+                fin = stream.tile([P, 512], F32, name="fin", tag="fin", bufs=2)
+                nc.vector.tensor_tensor(
+                    out=res[:], in0=out_banks[n][:], in1=ppb[:, 512 * n : 512 * n + 512], op=ALU.add
+                )
+                nc.scalar.activation(out=fin[:], in_=res[:], func=ACT.Relu)
+                nc.sync.dma_start(out=out_rows[:, 512 * n : 512 * n + 512], in_=fin[:])

@@ -18,11 +18,8 @@ P = 128
 B, N, NF = 4, 32, 1024
 GROUPS = 2
 M_TILES = 8
-CHUNKS = 8
+PAIRS = 16
 FLOPS = 2 * 4096 * NF * NF + 4 * 2 * 128 * NF * NF
-
-HALVES = (((2, "a"), (0, "g"), (1, "b"), (3, "g")), ((5, "a"), (4, "b"), (6, "g"), (7, "b")))
-LAST = (((2, "a"), (0, "g"), (1, "v"), (3, "g")), ((5, "g"), (4, "v"), (6, "b"), (7, "b")))
 
 
 def tile_compositionalkoopmanoperators_pa_w8_kernel(
@@ -34,7 +31,7 @@ def tile_compositionalkoopmanoperators_pa_w8_kernel(
         stream = ctx.enter_context(tc.tile_pool(name="stream", bufs=2))
         psum = ctx.enter_context(tc.psum_pool(name="psum", bufs=1))
 
-        rel_rows = rel_enc_bytes.rearrange("b i j k -> (b i j) k")
+        rel_rows = rel_enc_bytes.rearrange("b i j k -> (b i) j k")
         out_rows = out.rearrange("b i n -> (b i) n")
         rp_words = rp_w_words.rearrange("g p n t -> p g (n t)").bitcast(I32)
         pp_words = pp_w_words.rearrange("g p n t -> p g (n t)").bitcast(I32)
@@ -51,8 +48,6 @@ def tile_compositionalkoopmanoperators_pa_w8_kernel(
         obj_grp = keep.tile([P, GROUPS * 512], BF16, name="obj_grp", align_bytes=64)
         obj_codes = keep.tile([P, GROUPS * P], U32, name="obj_codes", align_bytes=64)
         obj_sc = keep.tile([P, GROUPS * P], U8, name="obj_sc", align_bytes=64)
-        srep_codes = keep.tile([P, B, GROUPS, 512], U32, name="srep_codes", align_bytes=64)
-        srep_sc = keep.tile([P, B, GROUPS, 512], U8, name="srep_sc", align_bytes=64)
         w_rel = [keep.tile([P, 2, 512], U32, name="w_rel%d" % h, align_bytes=64) for h in range(2)]
         w_obj = [keep.tile([P, 4, 512], U32, name="w_obj%d" % h, align_bytes=64) for h in range(2)]
         w_pp = keep.tile([P, 4, NF], U32, name="w_pp", align_bytes=64)
@@ -60,15 +55,13 @@ def tile_compositionalkoopmanoperators_pa_w8_kernel(
         pl_b = keep.tile([P, NF], U8, name="pl_b", align_bytes=64)
         pl_c = keep.tile([P, NF], U8, name="pl_c", align_bytes=64)
         recv = keep.tile([P, M_TILES, P], F32, name="recv")
-        neg_recv = keep.tile([P, M_TILES, P], F32, name="neg_recv")
-        split = keep.tile([P, M_TILES, P], F32, name="split")
         send = keep.tile([P, M_TILES, P], F32, name="send")
-        agg = keep.tile([P, M_TILES, P], F32, name="agg")
         agg_bf = keep.tile([P, 2, 512], BF16, name="agg_bf")
         agg_grp = keep.tile([P, 2, 512], BF16, name="agg_grp", align_bytes=64)
         agg_codes = keep.tile([P, 2, P], U32, name="agg_codes", align_bytes=64)
         agg_sc = keep.tile([P, 2, P], U8, name="agg_sc", align_bytes=64)
         warm = keep.tile([P, 1], F32, name="warm")
+        agg_bank = [psum.tile([P, 512], F32, name="agg%d" % h, tag="agg%d" % h, bufs=1) for h in range(2)]
 
         def w_codes(g, m):
             lo = (m % 4) * P
@@ -80,47 +73,43 @@ def tile_compositionalkoopmanoperators_pa_w8_kernel(
             return plane[4 * (g % 4) : P, m * P : m * P + P]
 
         raw, wide, xbank, grp, codes, scales, banks, sums = {}, {}, {}, {}, {}, {}, {}, {}
-        pending = {m: [] for m in range(M_TILES)}
 
         def e_bank():
-            bank = psum.tile([P, 512], F32, name="e_bank", tag="e", bufs=6)
+            bank = psum.tile([P, 512], F32, name="e_bank", tag="e", bufs=3)
             return bank
 
         def load(p):
             t = stream.tile([P, 2, NF], U8, name="rel_bytes", tag="rel_bytes", bufs=6)
-            src = rel_rows[256 * p : 256 * p + 256, :].rearrange("(s q) k -> q s k", q=P)
             if p == 0:
                 for s in range(2):
-                    nc.sync.dma_start(out=t[:, s, :], in_=src[:, s, :])
+                    nc.sync.dma_start(out=t[:, s, :], in_=rel_rows[:, s, :])
             else:
-                nc.sync.dma_start(out=t[:], in_=src)
+                nc.sync.dma_start(out=t[:], in_=rel_rows[:, 2 * p : 2 * p + 2, :])
             raw[p] = t
 
         def widen(p):
-            t = stream.tile([P, 2, NF], BF16, name="rel_wide", tag="rel_wide", bufs=3)
-            if p == 0:
-                for s in range(2):
+            t = stream.tile([P, 2, NF], BF16, name="rel_wide", tag="rel_wide", bufs=4)
+            for s in range(2):
+                if p == 0 and s == 1:
+                    nc.vector.tensor_copy(out=t[:, s, :], in_=raw[p][:, s, :].bitcast(FP8))
+                elif p < 4:
                     nc.scalar.copy(out=t[:, s, :], in_=raw[p][:, s, :].bitcast(FP8))
-            else:
-                nc.scalar.copy(
-                    out=t[:].rearrange("p s k -> p (s k)"),
-                    in_=raw[p][:].rearrange("p s k -> p (s k)").bitcast(FP8),
-                )
+                else:
+                    nc.gpsimd.tensor_copy(out=t[:, s, :], in_=raw[p][:, s, :].bitcast(FP8))
             wide[p] = t
 
-        def turn(p):
+        def turn(p, g):
             words = wide[p][:].bitcast(F32)
-            for g in range(GROUPS):
-                bank = psum.tile([P, 2, 256], F32, name="x%d" % g, tag="x%d" % g, bufs=1)
-                for s in range(2):
-                    for u in range(2):
-                        nc.tensor.transpose(
-                            bank[:, u, P * s : P * s + P], words[:, s, 256 * g + u : 256 * g + 256 : 2], ident[:]
-                        )
-                xbank[p, g] = bank
+            bank = psum.tile([P, 2, 256], F32, name="xbank", tag="x", bufs=3)
+            for s in range(2):
+                for u in range(2):
+                    nc.tensor.transpose(
+                        bank[:, u, P * s : P * s + P], words[:, s, 256 * g + u : 256 * g + 256 : 2], ident[:]
+                    )
+            xbank[p, g] = bank
 
         def scale_mul(p, g):
-            t = stream.tile([P, 256, 4], BF16, name="grp%d" % g, tag="grp%d" % g, bufs=2, align_bytes=64)
+            t = stream.tile([P, 256, 4], BF16, name="grp", tag="grp", bufs=4, align_bytes=64)
             src = xbank[p, g][:].rearrange("p u c -> p (u c)").bitcast(BF16)
             nc.vector.tensor_tensor(
                 out=t[:].rearrange("p c (u e) -> p c u e", u=2),
@@ -133,8 +122,8 @@ def tile_compositionalkoopmanoperators_pa_w8_kernel(
         def quant(p, g):
             c, h = p // 2, p % 2
             if c not in codes:
-                ct = stream.tile([P, GROUPS, 512], U32, name="codes", tag="codes", bufs=3, align_bytes=64)
-                st = stream.tile([P, GROUPS, 512], U8, name="scales", tag="scales", bufs=3, align_bytes=64)
+                ct = stream.tile([P, GROUPS, 512], U32, name="codes", tag="codes", bufs=4, align_bytes=64)
+                st = stream.tile([P, GROUPS, 512], U8, name="scales", tag="scales", bufs=4, align_bytes=64)
                 codes[c], scales[c] = ct, st
             cols = slice(256 * h, 256 * h + 256)
             nc.vector.quantize_mx(
@@ -143,93 +132,52 @@ def tile_compositionalkoopmanoperators_pa_w8_kernel(
                 in_=grp[p, g][:].rearrange("p c t -> p (c t)"),
             )
 
-        def replicate(b):
-            oc = obj_codes[:].bitcast(I32).rearrange("p (g o t) -> p g o t", g=GROUPS, o=1)
-            osc = obj_sc[:].bitcast(I32).rearrange("p (g o t) -> p g o t", g=GROUPS, o=1)
-            nc.vector.tensor_copy(
-                out=srep_codes[:, b].rearrange("p g (r j) -> p g r j", r=16).bitcast(I32),
-                in_=oc[:, :, :, 32 * b : 32 * b + 32].to_broadcast([P, GROUPS, 16, 32]),
-            )
-            nc.vector.tensor_copy(
-                out=srep_sc[:, b].rearrange("p g (r j) -> p g r j", r=16).bitcast(I32),
-                in_=osc[:, :, :, 8 * b : 8 * b + 8].to_broadcast([P, GROUPS, 16, 8]),
-            )
-
-        def products(c, m, mode):
-            b = c // 2
+        def products(c, m):
             bank = e_bank()
-            passes = []
-            if mode in "ab":
-                for g in range(GROUPS):
-                    passes.append((4 + g, srep_codes[:, b, g, :], srep_sc[:, b, g, :]))
             for g in range(GROUPS):
-                passes.append((g, codes[c][:, g, :], scales[c][:, g, :]))
-            for k, (g, mc, ms) in enumerate(passes):
                 nc.tensor.matmul_mx(
                     out=bank[:],
                     lhsT=w_codes(g, m),
                     lhsT_scale=w_scale(g, m),
-                    rhs=mc.bitcast(FP8X4),
-                    rhs_scale=ms,
-                    start=(k == 0),
-                    stop=(k == len(passes) - 1),
+                    rhs=codes[c][:, g, :].bitcast(FP8X4),
+                    rhs_scale=scales[c][:, g, :],
+                    start=(g == 0),
+                    stop=(g == 1),
                 )
             banks[c, m] = bank
 
-        def cols_of(c):
-            lo = 32 * (c // 2) + 16 * (c % 2)
-            return slice(lo, lo + 16)
-
-        def add_send(c, m):
-            b = c // 2
-            t = stream.tile([P, 16, 32], F32, name="sum_t", tag="sum_t", bufs=4)
+        def add_recv(c, m):
+            t = stream.tile([P, 4, P], F32, name="sum_t", tag="sum_t", bufs=14)
             nc.vector.tensor_tensor(
                 out=t[:],
-                in0=banks[c, m][:].rearrange("p (i j) -> p i j", i=16),
-                in1=send[:, m : m + 1, 32 * b : 32 * b + 32].to_broadcast([P, 16, 32]),
+                in0=banks[c, m][:].rearrange("p (j r) -> p j r", j=4),
+                in1=recv[:, m : m + 1, :].to_broadcast([P, 4, P]),
                 op=ALU.add,
             )
             sums[c, m] = t
 
-        def clip(c, m, mode):
-            src = banks[c, m][:].rearrange("p (i j) -> p i j", i=16) if mode == "b" else sums[c, m][:]
-            t = stream.tile([P, 16, 32], F32, name="clip_t", tag="clip_t", bufs=3)
-            nc.vector.tensor_tensor(
-                out=t[:],
-                in0=src,
-                in1=neg_recv[:, m, cols_of(c)].unsqueeze(2).to_broadcast([P, 16, 32]),
-                op=ALU.max,
-            )
-            sums[c, m] = t
+        def relu(c, m):
+            t = sums[c, m]
+            for j in range(4):
+                for b in range(B):
+                    col = 32 * b + 4 * c + j
+                    nc.scalar.activation(
+                        out=t[:, j, 32 * b : 32 * b + 32],
+                        in_=t[:, j, 32 * b : 32 * b + 32],
+                        func=ACT.Relu,
+                        bias=send[:, m, col : col + 1],
+                    )
 
-        def reduce_j(c, m):
-            nc.vector.tensor_reduce(out=agg[:, m, cols_of(c)], in_=sums[c, m][:], axis=AX.X, op=ALU.add)
-            pending[m].append(cols_of(c))
-
-        def undo(c, m):
-            if c % 2 == 1 and pending[m]:
-                cols = slice(pending[m][0].start, pending[m][-1].stop)
-                nc.vector.scalar_tensor_tensor(
-                    out=agg[:, m, cols],
-                    in0=neg_recv[:, m, cols],
-                    scalar=-32.0,
-                    in1=agg[:, m, cols],
-                    op0=ALU.mult,
-                    op1=ALU.add,
-                )
-                pending[m].clear()
-
-        def relu_sum(c, m, mode):
-            src = banks[c, m][:] if mode == "a" else sums[c, m][:].rearrange("p i j -> p (i j)")
-            junk = stream.tile([P, 512], BF16, name="junk", tag="junk", bufs=3)
-            lo = cols_of(c).start
-            for i in range(16):
-                nc.scalar.activation(
-                    out=junk[:, 32 * i : 32 * i + 32],
-                    in_=src[:, 32 * i : 32 * i + 32],
-                    func=ACT.Relu,
-                    bias=recv[:, m, lo + i : lo + i + 1],
-                    accum_out=agg[:, m, lo + i : lo + i + 1],
+        def collect(c, m):
+            for j in range(4):
+                k = m % 4
+                nc.tensor.matmul(
+                    agg_bank[m // 4][:, P * k : P * k + P],
+                    lhsT=sums[c, m][:, j, :],
+                    rhs=ident[:],
+                    is_transpose=True,
+                    start=(c == 0 and k == 0 and j == 0),
+                    stop=(c == 7 and k == 3 and j == 3),
                 )
 
         def obj_products(group, hf):
@@ -247,75 +195,66 @@ def tile_compositionalkoopmanoperators_pa_w8_kernel(
                     )
             return bank
 
-        def merge(a, b):
-            res = []
-            for k in range(max(len(a), len(b))):
-                if k < len(a):
-                    res.append(a[k])
-                if k < len(b):
-                    res.append(b[k])
-            return res
+        def add_send(c, m):
+            t = sums[c, m]
+            nc.vector.tensor_tensor(
+                out=t[:].rearrange("p j (b i) -> p j b i", b=B),
+                in0=t[:].rearrange("p j (b i) -> p j b i", b=B),
+                in1=send[:, m, :].rearrange("p (b j o) -> p j b o", b=B, o=1)[:, 4 * c : 4 * c + 4].to_broadcast([P, 4, B, 32]),
+                op=ALU.add,
+            )
 
-        def slot(s, tiles):
-            c = s // 2
-            prep = s + 2 < 16
-            for m, mode in tiles[:2]:
-                products(c, m, mode)
-            lanes = {"a": [], "g": [("A",)], "b": [("B",), ("C",)], "v": [("A",), ("B",), ("C",)]}
-            per = [[(op[0], m, mode) for op in lanes[mode]] for m, mode in tiles]
-            per = [x for x in per if x]
-            depth = max(len(x) for x in per)
-            order = []
-            for k in range(depth):
-                for x in per:
-                    if k < len(x):
-                        order.append(x[k])
-            pv = [("M", 0), ("M", 1), ("Q", 0), ("Q", 1)] if prep else []
-            emitted = [m for m, mode in tiles[:2]]
+        def relu_all(c, m):
+            t = sums[c, m]
+            nc.scalar.activation(out=t[:], in_=t[:], func=ACT.Relu)
 
-            def rest():
-                if s + 3 < 16:
-                    turn(s + 3)
-                for m, mode in tiles[2:]:
-                    products(c, m, mode)
-
-            for item in merge(pv, order):
-                if item[0] == "M":
-                    scale_mul(s + 2, item[1])
-                    continue
-                if item[0] == "Q":
-                    quant(s + 2, item[1])
-                    continue
-                if item[1] not in emitted:
-                    rest()
-                    emitted.extend([m for m, mode in tiles])
-                if item[0] == "A":
-                    add_send(c, item[1])
-                elif item[0] == "B":
-                    clip(c, item[1], item[2])
+        def slot(s):
+            c, h = s // 2, s % 2
+            tiles = [4 * h + k for k in range(4)]
+            long = [3] if s >= 13 else []
+            q, x, w = s + 3, s + 4, s + 5
+            for k in range(4):
+                products(c, tiles[k])
+                add_recv(c, tiles[k])
+            for k in long:
+                add_send(c, tiles[k])
+            if s == 0:
+                turn(3, 0)
+                turn(3, 1)
+            if q < PAIRS:
+                scale_mul(q, 0)
+                scale_mul(q, 1)
+                quant(q, 0)
+                quant(q, 1)
+            if s >= 1:
+                for k in range(4):
+                    collect((s - 1) // 2, 4 * ((s - 1) % 2) + k)
+            if w < PAIRS:
+                widen(w)
+            if x < PAIRS:
+                turn(x, 0)
+                turn(x, 1)
+            for k in range(4):
+                if k in long:
+                    relu_all(c, tiles[k])
                 else:
-                    reduce_j(c, item[1])
-                    undo(c, item[1])
-            first = True
-            for m, mode in tiles:
-                if mode in "ag":
-                    relu_sum(c, m, mode)
-                    if first and s + 4 < 16:
-                        widen(s + 4)
-                    first = False
+                    relu(c, tiles[k])
+            if s == 0:
+                receivers(1)
+                senders(1)
 
         with tc.manual_schedule():
             load(0)
             nc.sync.dma_start(
                 out=scale_sb[:], in_=rel_enc_scale.rearrange("a b c (g p t) -> p (a b c g) t", p=P, t=4)
             )
-            nc.sync.dma_start(out=obj_sb[:], in_=obj.rearrange("b i k -> (b i) k"))
             load(1)
+            nc.sync.dma_start(out=obj_sb[:], in_=obj.rearrange("b i k -> (b i) k"))
+            load(2)
+            nc.vector.memset(warm[:], 0.0)
             for plane in (pl_a, pl_b, pl_c):
                 nc.vector.memset(plane[:].bitcast(I32), 0)
-            nc.vector.memset(obj_sc[:].bitcast(I32), 0)
             nc.vector.memset(bias_row[:], 0.0)
-            nc.vector.memset(warm[:], 0.0)
             nc.scalar.activation(out=warm[:], in_=warm[:], func=ACT.Relu)
             for q in range(4):
                 nc.sync.dma_start(
@@ -327,17 +266,18 @@ def tile_compositionalkoopmanoperators_pa_w8_kernel(
                     out=pl_b[32 * q : 32 * q + 8, :].bitcast(I32),
                     in_=rp_w_scales[4:6, 4 * q : 4 * q + 4, :].bitcast(I32),
                 )
+            nc.sync.dma_start(out=bias_row[0:M_TILES, :], in_=rp_b.rearrange("(m p) -> m p", p=P))
             nc.sync.dma_start(out=w_obj[0][:].bitcast(I32), in_=rp_words[:, 2:6, 0:512])
             nc.sync.dma_start(out=w_rel[0][:].bitcast(I32), in_=rp_words[:, 0:2, 0:512])
-            nc.sync.dma_start(out=bias_row[0:M_TILES, :], in_=rp_b.rearrange("(m p) -> m p", p=P))
-            load(2)
-            nc.sync.dma_start(out=w_obj[1][:].bitcast(I32), in_=rp_words[:, 2:6, 512:1024])
-            nc.sync.dma_start(out=w_rel[1][:].bitcast(I32), in_=rp_words[:, 0:2, 512:1024])
             load(3)
             load(4)
+            nc.sync.dma_start(out=w_obj[1][:].bitcast(I32), in_=rp_words[:, 2:6, 512:1024])
+            nc.sync.dma_start(out=w_rel[1][:].bitcast(I32), in_=rp_words[:, 0:2, 512:1024])
+            load(5)
 
             widen(0)
-            turn(0)
+            turn(0, 0)
+            turn(0, 1)
             obj_bank = e_bank()
             obj_words = obj_sb[:].bitcast(F32)
             for g in range(GROUPS):
@@ -351,16 +291,19 @@ def tile_compositionalkoopmanoperators_pa_w8_kernel(
                 out=obj_grp[:].bitcast(F32).rearrange("p (g c u) -> p g c u", g=GROUPS, u=2),
                 in_=obj_bank[:].rearrange("p (g u c) -> p g c u", g=GROUPS, u=2),
             )
+            turn(1, 0)
             scale_mul(0, 0)
             scale_mul(0, 1)
             nc.vector.quantize_mx(out=obj_codes[:].bitcast(FP8X4), scales=obj_sc[:], in_=obj_grp[:])
+            turn(1, 1)
             quant(0, 0)
             quant(0, 1)
-            turn(1)
-            replicate(0)
-            scale_mul(1, 0)
-            scale_mul(1, 1)
             nc.vector.tensor_copy(out=bias_rowf[:], in_=bias_row[:])
+            widen(2)
+            scale_mul(1, 0)
+            turn(2, 0)
+            scale_mul(1, 1)
+            turn(2, 1)
             quant(1, 0)
             quant(1, 1)
             bias_bank = e_bank()
@@ -380,34 +323,20 @@ def tile_compositionalkoopmanoperators_pa_w8_kernel(
 
             def senders(hf):
                 bank = obj_products(4, hf)
-                nc.vector.tensor_copy(
-                    out=send[:, 4 * hf : 4 * hf + 4, :].rearrange("p m c -> p (m c)"), in_=bank[:]
-                )
+                nc.scalar.copy(out=send[:, 4 * hf : 4 * hf + 4, :].rearrange("p m c -> p (m c)"), in_=bank[:])
 
-            def negate(hf):
-                ms = slice(4 * hf, 4 * hf + 4)
-                nc.vector.scalar_tensor_tensor(
-                    out=split[:, ms, :], in0=recv[:, ms, :], scalar=33.0, in1=recv[:, ms, :],
-                    op0=ALU.mult, op1=ALU.subtract,
-                )
-                nc.vector.scalar_tensor_tensor(
-                    out=neg_recv[:, ms, :], in0=recv[:, ms, :], scalar=-33.0, in1=split[:, ms, :],
-                    op0=ALU.mult, op1=ALU.add,
-                )
-
+            scale_mul(2, 0)
+            scale_mul(2, 1)
+            quant(2, 0)
+            quant(2, 1)
             receivers(0)
             senders(0)
-            widen(2)
-            turn(2)
-            negate(0)
             widen(3)
-            receivers(1)
-            senders(1)
-            negate(1)
+            widen(4)
 
-            for s in range(16):
-                if s + 5 < 16:
-                    load(s + 5)
+            for s in range(PAIRS):
+                if s + 6 < PAIRS:
+                    load(s + 6)
                 if s == 1:
                     for q in range(4):
                         nc.sync.dma_start(
@@ -419,9 +348,7 @@ def tile_compositionalkoopmanoperators_pa_w8_kernel(
                     nc.sync.dma_start(out=w_pp[:, g, :].bitcast(I32), in_=pp_words[:, g, :])
                 if s == 9:
                     nc.sync.dma_start(out=ppb[:], in_=pp_b.partition_broadcast(P))
-                if s % 4 == 2 and s < 12:
-                    replicate(s // 4 + 1)
-                slot(s, (LAST if s >= 14 else HALVES)[s % 2])
+                slot(s)
 
             out_banks = [e_bank(), e_bank()]
 
@@ -439,28 +366,33 @@ def tile_compositionalkoopmanoperators_pa_w8_kernel(
 
             for g in range(GROUPS):
                 out_pass(obj_codes[:, P * g : P * g + P], obj_sc[:, P * g : P * g + P], g, g == 0, False)
-            for hf in range(2):
-                rows = e_bank()
-                for k in range(4):
-                    nc.tensor.transpose(rows[:, P * k : P * k + P], agg[:, 4 * hf + k, :], ident[:])
-                nc.vector.tensor_copy(out=agg_bf[:, hf, :], in_=rows[:])
+            def requantise(hf):
+                nc.vector.tensor_copy(out=agg_bf[:, hf, :], in_=agg_bank[hf][:])
                 agg_words = agg_bf[:, hf, :].bitcast(F32)
-                back = e_bank()
+                back = psum.tile([P, 2, 256], F32, name="xbank", tag="x", bufs=3)
                 for u in range(2):
-                    nc.tensor.transpose(back[:, P * u : P * u + P], agg_words[:, u:256:2], ident[:])
+                    nc.tensor.transpose(back[:, u, 0:P], agg_words[:, u:256:2], ident[:])
                 nc.vector.tensor_copy(
                     out=agg_grp[:, hf, :].bitcast(F32).rearrange("p (c u) -> p c u", u=2),
-                    in_=back[:, 0:256].rearrange("p (u c) -> p c u", u=2),
+                    in_=back[:, :, 0:P].rearrange("p u c -> p c u"),
                 )
                 nc.vector.quantize_mx(
                     out=agg_codes[:, hf, :].bitcast(FP8X4), scales=agg_sc[:, hf, :], in_=agg_grp[:, hf, :]
                 )
-                out_pass(agg_codes[:, hf, :], agg_sc[:, hf, :], 2 + hf, False, hf == 1)
+
+            requantise(0)
+            for k in range(4):
+                collect(7, 4 + k)
+            out_pass(agg_codes[:, 0, :], agg_sc[:, 0, :], 2, False, False)
+            requantise(1)
+            out_pass(agg_codes[:, 1, :], agg_sc[:, 1, :], 3, False, True)
             for n in range(2):
                 res = stream.tile([P, 512], F32, name="res", tag="res", bufs=2)
-                fin = stream.tile([P, 512], F32, name="fin", tag="fin", bufs=2)
                 nc.vector.tensor_tensor(
                     out=res[:], in0=out_banks[n][:], in1=ppb[:, 512 * n : 512 * n + 512], op=ALU.add
                 )
-                nc.scalar.activation(out=fin[:], in_=res[:], func=ACT.Relu)
-                nc.sync.dma_start(out=out_rows[:, 512 * n : 512 * n + 512], in_=fin[:])
+                if n == 0:
+                    nc.scalar.activation(out=res[:], in_=res[:], func=ACT.Relu)
+                else:
+                    nc.vector.tensor_scalar(out=res[:], in0=res[:], scalar1=0.0, scalar2=None, op0=ALU.max)
+                nc.sync.dma_start(out=out_rows[:, 512 * n : 512 * n + 512], in_=res[:])

@@ -12,13 +12,12 @@ FP8 = mybir.dt.float8_e4m3fn
 FP8X4 = mybir.dt.float8_e4m3fn_x4
 ALU = mybir.AluOpType
 ACT = mybir.ActivationFunctionType
-AX = mybir.AxisListType
 
 P = 128
 B, N, NF = 4, 32, 1024
 GROUPS = 2
 M_TILES = 8
-PAIRS = 16
+SLOTS = 16
 FLOPS = 2 * 4096 * NF * NF + 4 * 2 * 128 * NF * NF
 
 
@@ -46,8 +45,10 @@ def tile_compositionalkoopmanoperators_pa_w8_kernel(
         ppb = keep.tile([P, NF], BF16, name="ppb")
         obj_sb = keep.tile([P, NF], BF16, name="obj_sb")
         obj_grp = keep.tile([P, GROUPS * 512], BF16, name="obj_grp", align_bytes=64)
-        obj_codes = keep.tile([P, GROUPS * P], U32, name="obj_codes", align_bytes=64)
-        obj_sc = keep.tile([P, GROUPS * P], U8, name="obj_sc", align_bytes=64)
+        obj_codes = keep.tile([P, GROUPS, P], U32, name="obj_codes", align_bytes=64)
+        obj_sc = keep.tile([P, GROUPS, P], U8, name="obj_sc", align_bytes=64)
+        rep_codes = keep.tile([P, GROUPS, 512], U32, name="rep_codes", align_bytes=64)
+        rep_sc = keep.tile([P, GROUPS, 512], U8, name="rep_sc", align_bytes=64)
         w_rel = [keep.tile([P, 2, 512], U32, name="w_rel%d" % h, align_bytes=64) for h in range(2)]
         w_obj = [keep.tile([P, 4, 512], U32, name="w_obj%d" % h, align_bytes=64) for h in range(2)]
         w_pp = keep.tile([P, 4, NF], U32, name="w_pp", align_bytes=64)
@@ -61,7 +62,10 @@ def tile_compositionalkoopmanoperators_pa_w8_kernel(
         agg_codes = keep.tile([P, 2, P], U32, name="agg_codes", align_bytes=64)
         agg_sc = keep.tile([P, 2, P], U8, name="agg_sc", align_bytes=64)
         warm = keep.tile([P, 1], F32, name="warm")
+        token = keep.tile([P, 1], U32, name="token")
         agg_bank = [psum.tile([P, 512], F32, name="agg%d" % h, tag="agg%d" % h, bufs=1) for h in range(2)]
+
+        raw, wide, xbank, grp, codes, scales, banks, sums = {}, {}, {}, {}, {}, {}, {}, {}
 
         def w_codes(g, m):
             lo = (m % 4) * P
@@ -72,11 +76,17 @@ def tile_compositionalkoopmanoperators_pa_w8_kernel(
             plane = pl_a if g < 4 else pl_b
             return plane[4 * (g % 4) : P, m * P : m * P + P]
 
-        raw, wide, xbank, grp, codes, scales, banks, sums = {}, {}, {}, {}, {}, {}, {}, {}
-
         def e_bank():
             bank = psum.tile([P, 512], F32, name="e_bank", tag="e", bufs=3)
             return bank
+
+        def x_bank():
+            bank = psum.tile([P, 2, 256], F32, name="x_bank", tag="x", bufs=3)
+            return bank
+
+        def sum_tile():
+            t = stream.tile([P, 4, P], F32, name="sum_t", tag="sum_t", bufs=14)
+            return t
 
         def load(p):
             t = stream.tile([P, 2, NF], U8, name="rel_bytes", tag="rel_bytes", bufs=6)
@@ -88,19 +98,21 @@ def tile_compositionalkoopmanoperators_pa_w8_kernel(
             raw[p] = t
 
         def widen(p):
-            t = stream.tile([P, 2, NF], BF16, name="rel_wide", tag="rel_wide", bufs=4)
+            t = stream.tile([P, 2, NF], BF16, name="rel_wide", tag="rel_wide", bufs=3)
             for s in range(2):
+                src = raw[p][:, s, :].bitcast(FP8)
                 if p == 0 and s == 1:
-                    nc.vector.tensor_copy(out=t[:, s, :], in_=raw[p][:, s, :].bitcast(FP8))
+                    nc.vector.tensor_copy(out=t[:, s, :], in_=src)
                 elif p < 4:
-                    nc.scalar.copy(out=t[:, s, :], in_=raw[p][:, s, :].bitcast(FP8))
+                    nc.scalar.copy(out=t[:, s, :], in_=src)
                 else:
-                    nc.gpsimd.tensor_copy(out=t[:, s, :], in_=raw[p][:, s, :].bitcast(FP8))
+                    for a in range(0, NF, 1024):
+                        nc.gpsimd.tensor_copy(out=t[:, s, a : a + 1024], in_=src[:, a : a + 1024])
             wide[p] = t
 
         def turn(p, g):
             words = wide[p][:].bitcast(F32)
-            bank = psum.tile([P, 2, 256], F32, name="xbank", tag="x", bufs=3)
+            bank = x_bank()
             for s in range(2):
                 for u in range(2):
                     nc.tensor.transpose(
@@ -132,45 +144,85 @@ def tile_compositionalkoopmanoperators_pa_w8_kernel(
                 in_=grp[p, g][:].rearrange("p c t -> p (c t)"),
             )
 
-        def products(c, m):
+        def prepare(p, parts):
+            for part in parts:
+                if part == "M":
+                    scale_mul(p, 0)
+                    scale_mul(p, 1)
+                else:
+                    quant(p, 0)
+                    quant(p, 1)
+
+        def products(c, m, with_recv):
             bank = e_bank()
+            passes = []
+            if with_recv:
+                for g in range(GROUPS):
+                    passes.append((2 + g, rep_codes[:, g, :], rep_sc[:, g, :]))
             for g in range(GROUPS):
+                passes.append((g, codes[c][:, g, :], scales[c][:, g, :]))
+            for k, (g, mc, ms) in enumerate(passes):
                 nc.tensor.matmul_mx(
                     out=bank[:],
                     lhsT=w_codes(g, m),
                     lhsT_scale=w_scale(g, m),
-                    rhs=codes[c][:, g, :].bitcast(FP8X4),
-                    rhs_scale=scales[c][:, g, :],
-                    start=(g == 0),
-                    stop=(g == 1),
+                    rhs=mc.bitcast(FP8X4),
+                    rhs_scale=ms,
+                    start=(k == 0),
+                    stop=(k == len(passes) - 1),
                 )
             banks[c, m] = bank
 
+        def recv_cols(m):
+            return recv[:, m : m + 1, :].to_broadcast([P, 4, P])
+
+        def send_cols(c, m):
+            return send[:, m, :].rearrange("p (b j o) -> p j b o", b=B, o=1)[:, 4 * c : 4 * c + 4].to_broadcast(
+                [P, 4, B, N]
+            )
+
         def add_recv(c, m):
-            t = stream.tile([P, 4, P], F32, name="sum_t", tag="sum_t", bufs=14)
+            t = sum_tile()
             nc.vector.tensor_tensor(
-                out=t[:],
-                in0=banks[c, m][:].rearrange("p (j r) -> p j r", j=4),
-                in1=recv[:, m : m + 1, :].to_broadcast([P, 4, P]),
-                op=ALU.add,
+                out=t[:], in0=banks[c, m][:].rearrange("p (j r) -> p j r", j=4), in1=recv_cols(m), op=ALU.add
             )
             sums[c, m] = t
 
+        def lift_add_recv(c, m):
+            t = sum_tile()
+            nc.scalar.copy(out=t[:].rearrange("p j r -> p (j r)"), in_=banks[c, m][:])
+            nc.gpsimd.tensor_tensor(out=t[:], in0=t[:], in1=recv_cols(m), op=ALU.add)
+            sums[c, m] = t
+
+        def add_send(eng, c, m):
+            t = sums[c, m][:].rearrange("p j (b i) -> p j b i", b=B)
+            eng.tensor_tensor(out=t, in0=t, in1=send_cols(c, m), op=ALU.add)
+
         def relu(c, m):
             t = sums[c, m]
+            nc.scalar.activation(out=t[:], in_=t[:], func=ACT.Relu)
+
+        def send_relu(c, m, from_bank):
+            if from_bank:
+                t = sum_tile()
+                src = banks[c, m][:].rearrange("p (j r) -> p j r", j=4)
+                sums[c, m] = t
+            else:
+                t = sums[c, m]
+                src = t
             for j in range(4):
                 for b in range(B):
-                    col = 32 * b + 4 * c + j
+                    col = N * b + 4 * c + j
                     nc.scalar.activation(
-                        out=t[:, j, 32 * b : 32 * b + 32],
-                        in_=t[:, j, 32 * b : 32 * b + 32],
+                        out=t[:, j, N * b : N * b + N],
+                        in_=src[:, j, N * b : N * b + N],
                         func=ACT.Relu,
                         bias=send[:, m, col : col + 1],
                     )
 
         def collect(c, m):
+            k = m % 4
             for j in range(4):
-                k = m % 4
                 nc.tensor.matmul(
                     agg_bank[m // 4][:, P * k : P * k + P],
                     lhsT=sums[c, m][:, j, :],
@@ -180,6 +232,10 @@ def tile_compositionalkoopmanoperators_pa_w8_kernel(
                     stop=(c == 7 and k == 3 and j == 3),
                 )
 
+        def collect_slot(s):
+            for k in range(4):
+                collect(s // 2, 4 * (s % 2) + k)
+
         def obj_products(group, hf):
             bank = e_bank()
             for k in range(4):
@@ -188,60 +244,64 @@ def tile_compositionalkoopmanoperators_pa_w8_kernel(
                         out=bank[:, P * k : P * k + P],
                         lhsT=w_codes(group + g, 4 * hf + k),
                         lhsT_scale=w_scale(group + g, 4 * hf + k),
-                        rhs=obj_codes[:, P * g : P * g + P].bitcast(FP8X4),
-                        rhs_scale=obj_sc[:, P * g : P * g + P],
+                        rhs=obj_codes[:, g, :].bitcast(FP8X4),
+                        rhs_scale=obj_sc[:, g, :],
                         start=(g == 0),
                         stop=(g == 1),
                     )
             return bank
 
-        def add_send(c, m):
-            t = sums[c, m]
-            nc.vector.tensor_tensor(
-                out=t[:].rearrange("p j (b i) -> p j b i", b=B),
-                in0=t[:].rearrange("p j (b i) -> p j b i", b=B),
-                in1=send[:, m, :].rearrange("p (b j o) -> p j b o", b=B, o=1)[:, 4 * c : 4 * c + 4].to_broadcast([P, 4, B, 32]),
-                op=ALU.add,
-            )
+        def receivers(hf):
+            bank = obj_products(2, hf)
+            nc.scalar.copy(out=recv[:, 4 * hf : 4 * hf + 4, :].rearrange("p m c -> p (m c)"), in_=bank[:])
 
-        def relu_all(c, m):
-            t = sums[c, m]
-            nc.scalar.activation(out=t[:], in_=t[:], func=ACT.Relu)
+        def senders(hf):
+            bank = obj_products(4, hf)
+            for k in range(4):
+                m = 4 * hf + k
+                nc.scalar.activation(
+                    out=send[:, m, :], in_=bank[:, P * k : P * k + P], func=ACT.Identity, bias=bias_col[:, m : m + 1]
+                )
 
         def slot(s):
             c, h = s // 2, s % 2
             tiles = [4 * h + k for k in range(4)]
-            long = [3] if s >= 13 else []
-            q, x, w = s + 3, s + 4, s + 5
-            for k in range(4):
-                products(c, tiles[k])
-                add_recv(c, tiles[k])
-            for k in long:
-                add_send(c, tiles[k])
-            if s == 0:
-                turn(3, 0)
-                turn(3, 1)
-            if q < PAIRS:
-                scale_mul(q, 0)
-                scale_mul(q, 1)
-                quant(q, 0)
-                quant(q, 1)
-            if s >= 1:
-                for k in range(4):
-                    collect((s - 1) // 2, 4 * ((s - 1) % 2) + k)
-            if w < PAIRS:
-                widen(w)
-            if x < PAIRS:
-                turn(x, 0)
-                turn(x, 1)
-            for k in range(4):
-                if k in long:
-                    relu_all(c, tiles[k])
-                else:
-                    relu(c, tiles[k])
-            if s == 0:
-                receivers(1)
-                senders(1)
+            late = s >= 13
+            v_long = [tiles[k] for k in [3]] if late else []
+            g_long = [tiles[k] for k in [1]] if late else []
+            lifted = [tiles[3]] if 1 <= s < 13 else []
+            for m in tiles:
+                products(c, m, False)
+            for m in tiles:
+                if m not in lifted:
+                    add_recv(c, m)
+            for m in v_long:
+                add_send(nc.vector, c, m)
+            for m in g_long:
+                add_send(nc.gpsimd, c, m)
+            if s + 3 < SLOTS:
+                prepare(s + 3, "MQ")
+            for r in {13: [12], 14: [], 15: [13,14]}.get(s, [s - 1]):
+                collect_slot(r)
+            if s + 4 < SLOTS:
+                turn(s + 4, 0)
+                turn(s + 4, 1)
+            short = [m for m in tiles if m not in lifted and m not in v_long and m not in g_long]
+            for n in range(len(short)):
+                if n == 1:
+                    for m in lifted:
+                        lift_add_recv(c, m)
+                send_relu(c, short[n], False)
+            for m in lifted:
+                send_relu(c, m, False)
+            for m in g_long + v_long:
+                relu(c, m)
+            if s + 5 < SLOTS:
+                p = s + 3
+                nc.gpsimd.tensor_copy(
+                    out=token[:].bitcast(I32), in_=codes[p // 2][:, 1, 256 * (p % 2) : 256 * (p % 2) + 1].bitcast(I32)
+                )
+                widen(s + 5)
 
         with tc.manual_schedule():
             load(0)
@@ -255,6 +315,7 @@ def tile_compositionalkoopmanoperators_pa_w8_kernel(
             for plane in (pl_a, pl_b, pl_c):
                 nc.vector.memset(plane[:].bitcast(I32), 0)
             nc.vector.memset(bias_row[:], 0.0)
+            nc.vector.memset(obj_sc[:].rearrange("p g c -> p (g c)").bitcast(I32), 0)
             nc.scalar.activation(out=warm[:], in_=warm[:], func=ACT.Relu)
             for q in range(4):
                 nc.sync.dma_start(
@@ -292,50 +353,49 @@ def tile_compositionalkoopmanoperators_pa_w8_kernel(
                 in_=obj_bank[:].rearrange("p (g u c) -> p g c u", g=GROUPS, u=2),
             )
             turn(1, 0)
-            scale_mul(0, 0)
-            scale_mul(0, 1)
-            nc.vector.quantize_mx(out=obj_codes[:].bitcast(FP8X4), scales=obj_sc[:], in_=obj_grp[:])
-            turn(1, 1)
-            quant(0, 0)
-            quant(0, 1)
+            prepare(0, "M")
+            nc.vector.quantize_mx(
+                out=obj_codes[:].rearrange("p g c -> p (g c)").bitcast(FP8X4),
+                scales=obj_sc[:].rearrange("p g c -> p (g c)"),
+                in_=obj_grp[:],
+            )
+            prepare(0, "Q")
             nc.vector.tensor_copy(out=bias_rowf[:], in_=bias_row[:])
+            turn(1, 1)
             widen(2)
-            scale_mul(1, 0)
+            prepare(1, "M")
             turn(2, 0)
-            scale_mul(1, 1)
             turn(2, 1)
-            quant(1, 0)
-            quant(1, 1)
+            prepare(1, "Q")
             bias_bank = e_bank()
             nc.tensor.transpose(bias_bank[:, 0:P], bias_rowf[:], ident[:])
             nc.scalar.copy(out=bias_col[:], in_=bias_bank[:, 0:M_TILES])
-
-            def receivers(hf):
-                bank = obj_products(2, hf)
-                for k in range(4):
-                    m = 4 * hf + k
-                    nc.scalar.activation(
-                        out=recv[:, m, :],
-                        in_=bank[:, P * k : P * k + P],
-                        func=ACT.Identity,
-                        bias=bias_col[:, m : m + 1],
-                    )
-
-            def senders(hf):
-                bank = obj_products(4, hf)
-                nc.scalar.copy(out=send[:, 4 * hf : 4 * hf + 4, :].rearrange("p m c -> p (m c)"), in_=bank[:])
-
-            scale_mul(2, 0)
-            scale_mul(2, 1)
-            quant(2, 0)
-            quant(2, 1)
             receivers(0)
             senders(0)
             widen(3)
+            for m in range(4):
+                products(0, m, False)
+            turn(3, 0)
+            turn(3, 1)
+            prepare(2, "M")
+            for m in range(4):
+                add_recv(0, m)
+            prepare(2, "Q")
             widen(4)
+            send_relu(0, 0, False)
+            send_relu(0, 1, False)
+            receivers(1)
+            senders(1)
+            prepare(3, "MQ")
+            send_relu(0, 2, False)
+            send_relu(0, 3, False)
+            turn(4, 0)
+            turn(4, 1)
+            widen(5)
+            load(6)
 
-            for s in range(PAIRS):
-                if s + 6 < PAIRS:
+            for s in range(1, SLOTS):
+                if s + 6 < SLOTS:
                     load(s + 6)
                 if s == 1:
                     for q in range(4):
@@ -364,12 +424,12 @@ def tile_compositionalkoopmanoperators_pa_w8_kernel(
                         stop=last,
                     )
 
-            for g in range(GROUPS):
-                out_pass(obj_codes[:, P * g : P * g + P], obj_sc[:, P * g : P * g + P], g, g == 0, False)
-            def requantise(hf):
+            def round_agg(hf):
                 nc.vector.tensor_copy(out=agg_bf[:, hf, :], in_=agg_bank[hf][:])
+
+            def requantise(hf):
                 agg_words = agg_bf[:, hf, :].bitcast(F32)
-                back = psum.tile([P, 2, 256], F32, name="xbank", tag="x", bufs=3)
+                back = x_bank()
                 for u in range(2):
                     nc.tensor.transpose(back[:, u, 0:P], agg_words[:, u:256:2], ident[:])
                 nc.vector.tensor_copy(
@@ -380,19 +440,24 @@ def tile_compositionalkoopmanoperators_pa_w8_kernel(
                     out=agg_codes[:, hf, :].bitcast(FP8X4), scales=agg_sc[:, hf, :], in_=agg_grp[:, hf, :]
                 )
 
-            requantise(0)
-            for k in range(4):
+            round_agg(0)
+            for k in [0,1,2]:
                 collect(7, 4 + k)
-            out_pass(agg_codes[:, 0, :], agg_sc[:, 0, :], 2, False, False)
+            requantise(0)
+            collect(7, 7)
+            round_agg(1)
+            for g in range(GROUPS):
+                out_pass(obj_codes[:, g, :], obj_sc[:, g, :], g, g == 0, False)
             requantise(1)
+            out_pass(agg_codes[:, 0, :], agg_sc[:, 0, :], 2, False, False)
             out_pass(agg_codes[:, 1, :], agg_sc[:, 1, :], 3, False, True)
-            for n in range(2):
-                res = stream.tile([P, 512], F32, name="res", tag="res", bufs=2)
-                nc.vector.tensor_tensor(
-                    out=res[:], in0=out_banks[n][:], in1=ppb[:, 512 * n : 512 * n + 512], op=ALU.add
-                )
-                if n == 0:
+            for n in range(4):
+                cols = slice(256 * (n % 2), 256 * (n % 2) + 256)
+                dest = slice(256 * n, 256 * n + 256)
+                res = stream.tile([P, 256], F32, name="res", tag="res", bufs=4)
+                nc.vector.tensor_tensor(out=res[:], in0=out_banks[n // 2][:, cols], in1=ppb[:, dest], op=ALU.add)
+                if n < 3:
                     nc.scalar.activation(out=res[:], in_=res[:], func=ACT.Relu)
                 else:
                     nc.vector.tensor_scalar(out=res[:], in0=res[:], scalar1=0.0, scalar2=None, op0=ALU.max)
-                nc.sync.dma_start(out=out_rows[:, 512 * n : 512 * n + 512], in_=res[:])
+                nc.sync.dma_start(out=out_rows[:, dest], in_=res[:])

@@ -15,10 +15,17 @@ ACT = mybir.ActivationFunctionType
 
 P = 128
 B, N, NF = 4, 32, 1024
-GROUPS = 2
-M_TILES = 8
-SLOTS = 16
-FLOPS = 2 * 4096 * NF * NF + 4 * 2 * 128 * NF * NF
+T = 4
+GROUPS = NF // (P * T)
+M_TILES = NF // P
+HALF = M_TILES // 2
+PAIRS = N // 2
+CHUNKS = N // 4
+SLOTS = 2 * CHUNKS
+COLS = 4 * P
+REL, RECV, SEND = 0, 2, 4
+
+FLOPS = 2 * B * N * N * NF * NF + 4 * 2 * B * N * NF * NF
 
 
 def tile_compositionalkoopmanoperators_pa_w8_kernel(
@@ -38,309 +45,311 @@ def tile_compositionalkoopmanoperators_pa_w8_kernel(
         ident = keep.tile([P, P], F32, name="ident")
         make_identity(nc, ident[:])
 
-        scale_sb = keep.tile([P, GROUPS, 4], F32, name="scale_sb")
+        rel_scale = keep.tile([P, GROUPS, T], F32, name="rel_scale")
         bias_row = keep.tile([P, P], BF16, name="bias_row")
-        bias_rowf = keep.tile([P, P], F32, name="bias_rowf")
+        bias_row_f32 = keep.tile([P, P], F32, name="bias_row_f32")
         bias_col = keep.tile([P, M_TILES], F32, name="bias_col")
-        ppb = keep.tile([P, NF], BF16, name="ppb")
-        obj_sb = keep.tile([P, NF], BF16, name="obj_sb")
-        obj_grp = keep.tile([P, GROUPS * 512], BF16, name="obj_grp", align_bytes=64)
-        obj_codes = keep.tile([P, GROUPS, P], U32, name="obj_codes", align_bytes=64)
-        obj_sc = keep.tile([P, GROUPS, P], U8, name="obj_sc", align_bytes=64)
-        rep_codes = keep.tile([P, GROUPS, 512], U32, name="rep_codes", align_bytes=64)
-        rep_sc = keep.tile([P, GROUPS, 512], U8, name="rep_sc", align_bytes=64)
-        w_rel = [keep.tile([P, 2, 512], U32, name="w_rel%d" % h, align_bytes=64) for h in range(2)]
-        w_obj = [keep.tile([P, 4, 512], U32, name="w_obj%d" % h, align_bytes=64) for h in range(2)]
+        out_bias = keep.tile([P, NF], BF16, name="out_bias")
+        obj_rows = keep.tile([P, NF], BF16, name="obj_rows")
+        obj_grouped = keep.tile([P, GROUPS * P * T], BF16, name="obj_grouped", align_bytes=64)
+        obj_codes = keep.tile([P, GROUPS * P], U32, name="obj_codes", align_bytes=64)
+        obj_scales = keep.tile([P, GROUPS * P], U8, name="obj_scales", align_bytes=64)
+        w_rel = [keep.tile([P, 2, NF // 2], U32, name="w_rel%d" % h, align_bytes=64) for h in range(2)]
+        w_obj = [keep.tile([P, 4, NF // 2], U32, name="w_obj%d" % h, align_bytes=64) for h in range(2)]
         w_pp = keep.tile([P, 4, NF], U32, name="w_pp", align_bytes=64)
-        pl_a = keep.tile([P, NF], U8, name="pl_a", align_bytes=64)
-        pl_b = keep.tile([P, NF], U8, name="pl_b", align_bytes=64)
-        pl_c = keep.tile([P, NF], U8, name="pl_c", align_bytes=64)
+        rp_plane_low = keep.tile([P, NF], U8, name="rp_plane_low", align_bytes=64)
+        rp_plane_high = keep.tile([P, NF], U8, name="rp_plane_high", align_bytes=64)
+        pp_plane = keep.tile([P, NF], U8, name="pp_plane", align_bytes=64)
         recv = keep.tile([P, M_TILES, P], F32, name="recv")
         send = keep.tile([P, M_TILES, P], F32, name="send")
-        agg_bf = keep.tile([P, 2, 512], BF16, name="agg_bf")
-        agg_grp = keep.tile([P, 2, 512], BF16, name="agg_grp", align_bytes=64)
+        agg_rows = keep.tile([P, 2, NF // 2], BF16, name="agg_rows")
+        agg_grouped = keep.tile([P, 2, P * T], BF16, name="agg_grouped", align_bytes=64)
         agg_codes = keep.tile([P, 2, P], U32, name="agg_codes", align_bytes=64)
-        agg_sc = keep.tile([P, 2, P], U8, name="agg_sc", align_bytes=64)
-        warm = keep.tile([P, 1], F32, name="warm")
-        token = keep.tile([P, 1], U32, name="token")
-        agg_bank = [psum.tile([P, 512], F32, name="agg%d" % h, tag="agg%d" % h, bufs=1) for h in range(2)]
+        agg_scales = keep.tile([P, 2, P], U8, name="agg_scales", align_bytes=64)
+        table_warmer = keep.tile([P, 1], F32, name="table_warmer")
+        turn_token = keep.tile([P, 1], U32, name="turn_token")
+        agg_bank = [psum.tile([P, NF // 2], F32, name="agg%d" % h, tag="agg%d" % h, bufs=1) for h in range(2)]
 
-        raw, wide, xbank, grp, codes, scales, banks, sums = {}, {}, {}, {}, {}, {}, {}, {}
-
-        def w_codes(g, m):
-            lo = (m % 4) * P
-            tile = w_rel[m // 4][:, g, lo : lo + P] if g < 2 else w_obj[m // 4][:, g - 2, lo : lo + P]
-            return tile.bitcast(FP8X4)
-
-        def w_scale(g, m):
-            plane = pl_a if g < 4 else pl_b
-            return plane[4 * (g % 4) : P, m * P : m * P + P]
-
-        def e_bank():
-            bank = psum.tile([P, 512], F32, name="e_bank", tag="e", bufs=3)
+        def product_bank():
+            bank = psum.tile([P, COLS], F32, name="product_bank", tag="product_bank", bufs=3)
             return bank
 
-        def x_bank():
-            bank = psum.tile([P, 2, 256], F32, name="x_bank", tag="x", bufs=3)
+        def turned_bank():
+            bank = psum.tile([P, 2, 2 * P], F32, name="turned_bank", tag="turned_bank", bufs=3)
             return bank
 
-        def sum_tile():
-            t = stream.tile([P, 4, P], F32, name="sum_t", tag="sum_t", bufs=14)
-            return t
+        rel_bytes, rel_wide, turned, grouped, codes, scales, products, effects = {}, {}, {}, {}, {}, {}, {}, {}
+
 
         def load(p):
             t = stream.tile([P, 2, NF], U8, name="rel_bytes", tag="rel_bytes", bufs=6)
             if p == 0:
-                for s in range(2):
-                    nc.sync.dma_start(out=t[:, s, :], in_=rel_rows[:, s, :])
+                for j in range(2):
+                    nc.sync.dma_start(out=t[:, j, :], in_=rel_rows[:, j, :])
             else:
                 nc.sync.dma_start(out=t[:], in_=rel_rows[:, 2 * p : 2 * p + 2, :])
-            raw[p] = t
+            rel_bytes[p] = t
 
         def widen(p):
             t = stream.tile([P, 2, NF], BF16, name="rel_wide", tag="rel_wide", bufs=3)
-            for s in range(2):
-                src = raw[p][:, s, :].bitcast(FP8)
-                if p == 0 and s == 1:
-                    nc.vector.tensor_copy(out=t[:, s, :], in_=src)
+            for j in range(2):
+                values = rel_bytes[p][:, j, :].bitcast(FP8)
+                if p == 0 and j == 1:
+                    nc.vector.tensor_copy(out=t[:, j, :], in_=values)
                 elif p < 4:
-                    nc.scalar.copy(out=t[:, s, :], in_=src)
+                    nc.scalar.copy(out=t[:, j, :], in_=values)
                 else:
-                    for a in range(0, NF, 1024):
-                        nc.gpsimd.tensor_copy(out=t[:, s, a : a + 1024], in_=src[:, a : a + 1024])
-            wide[p] = t
+                    nc.gpsimd.tensor_copy(out=t[:, j, :], in_=values)
+            rel_wide[p] = t
 
         def turn(p, g):
-            words = wide[p][:].bitcast(F32)
-            bank = x_bank()
-            for s in range(2):
+            words = rel_wide[p][:].bitcast(F32)
+            bank = turned_bank()
+            for j in range(2):
                 for u in range(2):
                     nc.tensor.transpose(
-                        bank[:, u, P * s : P * s + P], words[:, s, 256 * g + u : 256 * g + 256 : 2], ident[:]
+                        bank[:, u, P * j : P * j + P], words[:, j, 256 * g + u : 256 * g + 256 : 2], ident[:]
                     )
-            xbank[p, g] = bank
+            turned[p, g] = bank
 
-        def scale_mul(p, g):
-            t = stream.tile([P, 256, 4], BF16, name="grp", tag="grp", bufs=4, align_bytes=64)
-            src = xbank[p, g][:].rearrange("p u c -> p (u c)").bitcast(BF16)
+        def scale(p, g):
+            t = stream.tile([P, 2 * P, T], BF16, name="grouped", tag="grouped", bufs=4, align_bytes=64)
+            values = turned[p, g][:].rearrange("p u c -> p (u c)").bitcast(BF16)
             nc.vector.tensor_tensor(
                 out=t[:].rearrange("p c (u e) -> p c u e", u=2),
-                in0=src.rearrange("p (u c e) -> p c u e", u=2, e=2),
-                in1=scale_sb[:, g, :].rearrange("p (o u e) -> p o u e", o=1, u=2).to_broadcast([P, 256, 2, 2]),
+                in0=values.rearrange("p (u c e) -> p c u e", u=2, e=2),
+                in1=rel_scale[:, g, :].rearrange("p (o u e) -> p o u e", o=1, u=2).to_broadcast([P, 2 * P, 2, 2]),
                 op=ALU.mult,
             )
-            grp[p, g] = t
+            grouped[p, g] = t
 
-        def quant(p, g):
+        def quantise(p, g):
             c, h = p // 2, p % 2
             if c not in codes:
-                ct = stream.tile([P, GROUPS, 512], U32, name="codes", tag="codes", bufs=4, align_bytes=64)
-                st = stream.tile([P, GROUPS, 512], U8, name="scales", tag="scales", bufs=4, align_bytes=64)
-                codes[c], scales[c] = ct, st
-            cols = slice(256 * h, 256 * h + 256)
+                code_tile = stream.tile([P, GROUPS, COLS], U32, name="codes", tag="codes", bufs=4, align_bytes=64)
+                scale_tile = stream.tile([P, GROUPS, COLS], U8, name="scales", tag="scales", bufs=4, align_bytes=64)
+                codes[c], scales[c] = code_tile, scale_tile
+            cols = slice(2 * P * h, 2 * P * h + 2 * P)
             nc.vector.quantize_mx(
                 out=codes[c][:, g, cols].bitcast(FP8X4),
                 scales=scales[c][:, g, cols],
-                in_=grp[p, g][:].rearrange("p c t -> p (c t)"),
+                in_=grouped[p, g][:].rearrange("p c t -> p (c t)"),
             )
 
-        def prepare(p, parts):
-            for part in parts:
-                if part == "M":
-                    scale_mul(p, 0)
-                    scale_mul(p, 1)
-                else:
-                    quant(p, 0)
-                    quant(p, 1)
 
-        def products(c, m, with_recv):
-            bank = e_bank()
-            passes = []
-            if with_recv:
-                for g in range(GROUPS):
-                    passes.append((2 + g, rep_codes[:, g, :], rep_sc[:, g, :]))
+        def weight(g, m):
+            lo = (m % HALF) * P
+            if g < RECV:
+                words = w_rel[m // HALF][:, g, lo : lo + P]
+            else:
+                words = w_obj[m // HALF][:, g - RECV, lo : lo + P]
+            plane = rp_plane_low if g < SEND else rp_plane_high
+            return words.bitcast(FP8X4), plane[4 * (g % 4) : P, m * P : m * P + P]
+
+        def multiply(c, m):
+            bank = product_bank()
             for g in range(GROUPS):
-                passes.append((g, codes[c][:, g, :], scales[c][:, g, :]))
-            for k, (g, mc, ms) in enumerate(passes):
+                w, w_scale = weight(REL + g, m)
                 nc.tensor.matmul_mx(
                     out=bank[:],
-                    lhsT=w_codes(g, m),
-                    lhsT_scale=w_scale(g, m),
-                    rhs=mc.bitcast(FP8X4),
-                    rhs_scale=ms,
-                    start=(k == 0),
-                    stop=(k == len(passes) - 1),
+                    lhsT=w,
+                    lhsT_scale=w_scale,
+                    rhs=codes[c][:, g, :].bitcast(FP8X4),
+                    rhs_scale=scales[c][:, g, :],
+                    start=(g == 0),
+                    stop=(g == GROUPS - 1),
                 )
-            banks[c, m] = bank
+            products[c, m] = bank
 
-        def recv_cols(m):
+        def effect_tile():
+            t = stream.tile([P, 4, P], F32, name="effect", tag="effect", bufs=14)
+            return t
+
+        def recv_columns(m):
             return recv[:, m : m + 1, :].to_broadcast([P, 4, P])
 
-        def send_cols(c, m):
-            return send[:, m, :].rearrange("p (b j o) -> p j b o", b=B, o=1)[:, 4 * c : 4 * c + 4].to_broadcast(
-                [P, 4, B, N]
-            )
-
-        def add_recv(c, m):
-            t = sum_tile()
+        def add_receiver(c, m):
+            t = effect_tile()
             nc.vector.tensor_tensor(
-                out=t[:], in0=banks[c, m][:].rearrange("p (j r) -> p j r", j=4), in1=recv_cols(m), op=ALU.add
+                out=t[:], in0=products[c, m][:].rearrange("p (j r) -> p j r", j=4), in1=recv_columns(m), op=ALU.add
             )
-            sums[c, m] = t
+            effects[c, m] = t
 
-        def lift_add_recv(c, m):
-            t = sum_tile()
-            nc.scalar.copy(out=t[:].rearrange("p j r -> p (j r)"), in_=banks[c, m][:])
-            nc.gpsimd.tensor_tensor(out=t[:], in0=t[:], in1=recv_cols(m), op=ALU.add)
-            sums[c, m] = t
+        def lift_and_add_receiver(c, m):
+            t = effect_tile()
+            nc.scalar.copy(out=t[:].rearrange("p j r -> p (j r)"), in_=products[c, m][:])
+            nc.gpsimd.tensor_tensor(out=t[:], in0=t[:], in1=recv_columns(m), op=ALU.add)
+            effects[c, m] = t
 
-        def add_send(eng, c, m):
-            t = sums[c, m][:].rearrange("p j (b i) -> p j b i", b=B)
-            eng.tensor_tensor(out=t, in0=t, in1=send_cols(c, m), op=ALU.add)
-
-        def relu(c, m):
-            t = sums[c, m]
-            nc.scalar.activation(out=t[:], in_=t[:], func=ACT.Relu)
-
-        def send_relu(c, m, from_bank):
-            if from_bank:
-                t = sum_tile()
-                src = banks[c, m][:].rearrange("p (j r) -> p j r", j=4)
-                sums[c, m] = t
-            else:
-                t = sums[c, m]
-                src = t
+        def add_sender_and_relu(c, m):
+            t = effects[c, m]
             for j in range(4):
                 for b in range(B):
-                    col = N * b + 4 * c + j
+                    sender = N * b + 4 * c + j
                     nc.scalar.activation(
                         out=t[:, j, N * b : N * b + N],
-                        in_=src[:, j, N * b : N * b + N],
+                        in_=t[:, j, N * b : N * b + N],
                         func=ACT.Relu,
-                        bias=send[:, m, col : col + 1],
+                        bias=send[:, m, sender : sender + 1],
                     )
 
+        def add_sender(c, m):
+            t = effects[c, m][:].rearrange("p j (b i) -> p j b i", b=B)
+            terms = send[:, m, :].rearrange("p (b j o) -> p j b o", b=B, o=1)[:, 4 * c : 4 * c + 4]
+            nc.vector.tensor_tensor(out=t, in0=t, in1=terms.to_broadcast([P, 4, B, N]), op=ALU.add)
+
+        def relu(c, m):
+            t = effects[c, m]
+            nc.scalar.activation(out=t[:], in_=t[:], func=ACT.Relu)
+
         def collect(c, m):
-            k = m % 4
+            k = m % HALF
             for j in range(4):
                 nc.tensor.matmul(
-                    agg_bank[m // 4][:, P * k : P * k + P],
-                    lhsT=sums[c, m][:, j, :],
+                    agg_bank[m // HALF][:, P * k : P * k + P],
+                    lhsT=effects[c, m][:, j, :],
                     rhs=ident[:],
                     is_transpose=True,
                     start=(c == 0 and k == 0 and j == 0),
-                    stop=(c == 7 and k == 3 and j == 3),
+                    stop=(c == CHUNKS - 1 and k == HALF - 1 and j == 3),
                 )
 
-        def collect_slot(s):
-            for k in range(4):
-                collect(s // 2, 4 * (s % 2) + k)
-
-        def obj_products(group, hf):
-            bank = e_bank()
-            for k in range(4):
+        def multiply_objects(group, h):
+            bank = product_bank()
+            for k in range(HALF):
                 for g in range(GROUPS):
+                    w, w_scale = weight(group + g, HALF * h + k)
                     nc.tensor.matmul_mx(
                         out=bank[:, P * k : P * k + P],
-                        lhsT=w_codes(group + g, 4 * hf + k),
-                        lhsT_scale=w_scale(group + g, 4 * hf + k),
-                        rhs=obj_codes[:, g, :].bitcast(FP8X4),
-                        rhs_scale=obj_sc[:, g, :],
+                        lhsT=w,
+                        lhsT_scale=w_scale,
+                        rhs=obj_codes[:, P * g : P * g + P].bitcast(FP8X4),
+                        rhs_scale=obj_scales[:, P * g : P * g + P],
                         start=(g == 0),
-                        stop=(g == 1),
+                        stop=(g == GROUPS - 1),
                     )
             return bank
 
-        def receivers(hf):
-            bank = obj_products(2, hf)
-            nc.scalar.copy(out=recv[:, 4 * hf : 4 * hf + 4, :].rearrange("p m c -> p (m c)"), in_=bank[:])
+        def receivers(h):
+            bank = multiply_objects(RECV, h)
+            nc.scalar.copy(out=recv[:, HALF * h : HALF * h + HALF, :].rearrange("p m c -> p (m c)"), in_=bank[:])
 
-        def senders(hf):
-            bank = obj_products(4, hf)
-            for k in range(4):
-                m = 4 * hf + k
+        def senders(h):
+            bank = multiply_objects(SEND, h)
+            for k in range(HALF):
+                m = HALF * h + k
                 nc.scalar.activation(
                     out=send[:, m, :], in_=bank[:, P * k : P * k + P], func=ACT.Identity, bias=bias_col[:, m : m + 1]
                 )
 
+        def slot_tiles(s):
+            return [(s // 2, HALF * (s % 2) + k) for k in range(HALF)]
+
         def slot(s):
-            c, h = s // 2, s % 2
-            tiles = [4 * h + k for k in range(4)]
-            late = s >= 13
-            v_long = [tiles[k] for k in [3]] if late else []
-            g_long = [tiles[k] for k in [1]] if late else []
-            lifted = [tiles[3]] if 1 <= s < 13 else []
-            for m in tiles:
-                products(c, m, False)
-            for m in tiles:
-                if m not in lifted:
-                    add_recv(c, m)
-            for m in v_long:
-                add_send(nc.vector, c, m)
-            for m in g_long:
-                add_send(nc.gpsimd, c, m)
-            if s + 3 < SLOTS:
-                prepare(s + 3, "MQ")
-            for r in {13: [12], 14: [], 15: [13,14]}.get(s, [s - 1]):
-                collect_slot(r)
-            if s + 4 < SLOTS:
+            tiles = slot_tiles(s)
+            preparing = s + 3 < PAIRS
+            lifted = tiles[HALF - 1]
+            for tile in tiles:
+                multiply(*tile)
+            for tile in tiles:
+                if tile != lifted or not preparing:
+                    add_receiver(*tile)
+            if preparing:
+                scale(s + 3, 0)
+                scale(s + 3, 1)
+                quantise(s + 3, 0)
+                quantise(s + 3, 1)
+            else:
+                add_sender(*lifted)
+            for tile in slot_tiles(s - 1):
+                collect(*tile)
+            if s + 4 < PAIRS:
                 turn(s + 4, 0)
                 turn(s + 4, 1)
-            short = [m for m in tiles if m not in lifted and m not in v_long and m not in g_long]
-            for n in range(len(short)):
-                if n == 1:
-                    for m in lifted:
-                        lift_add_recv(c, m)
-                send_relu(c, short[n], False)
-            for m in lifted:
-                send_relu(c, m, False)
-            for m in g_long + v_long:
-                relu(c, m)
-            if s + 5 < SLOTS:
-                p = s + 3
+            add_sender_and_relu(*tiles[0])
+            if preparing:
+                lift_and_add_receiver(*lifted)
+            add_sender_and_relu(*tiles[1])
+            add_sender_and_relu(*tiles[2])
+            if preparing:
+                add_sender_and_relu(*lifted)
+            else:
+                relu(*lifted)
+            if s + 5 < PAIRS:
+                c, h = (s + 3) // 2, (s + 3) % 2
                 nc.gpsimd.tensor_copy(
-                    out=token[:].bitcast(I32), in_=codes[p // 2][:, 1, 256 * (p % 2) : 256 * (p % 2) + 1].bitcast(I32)
+                    out=turn_token[:].bitcast(I32), in_=codes[c][:, 0, 2 * P * h : 2 * P * h + 1].bitcast(I32)
                 )
                 widen(s + 5)
+
+
+        def multiply_out(banks, act_codes, act_scales, g, first, last):
+            for n in range(2):
+                cols = slice(COLS * n, COLS * n + COLS)
+                nc.tensor.matmul_mx(
+                    out=banks[n][:],
+                    lhsT=act_codes.bitcast(FP8X4),
+                    lhsT_scale=act_scales,
+                    rhs=w_pp[:, g, cols].bitcast(FP8X4),
+                    rhs_scale=pp_plane[4 * g : P, cols],
+                    start=first,
+                    stop=last,
+                )
+
+        def round_agg(h):
+            nc.vector.tensor_copy(out=agg_rows[:, h, :], in_=agg_bank[h][:])
+
+        def quantise_agg(h):
+            words = agg_rows[:, h, :].bitcast(F32)
+            bank = turned_bank()
+            for u in range(2):
+                nc.tensor.transpose(bank[:, u, 0:P], words[:, u : 2 * P : 2], ident[:])
+            nc.vector.tensor_copy(
+                out=agg_grouped[:, h, :].bitcast(F32).rearrange("p (c u) -> p c u", u=2),
+                in_=bank[:, :, 0:P].rearrange("p u c -> p c u"),
+            )
+            nc.vector.quantize_mx(
+                out=agg_codes[:, h, :].bitcast(FP8X4), scales=agg_scales[:, h, :], in_=agg_grouped[:, h, :]
+            )
 
         with tc.manual_schedule():
             load(0)
             nc.sync.dma_start(
-                out=scale_sb[:], in_=rel_enc_scale.rearrange("a b c (g p t) -> p (a b c g) t", p=P, t=4)
+                out=rel_scale[:], in_=rel_enc_scale.rearrange("a b c (g p t) -> p (a b c g) t", p=P, t=T)
             )
             load(1)
-            nc.sync.dma_start(out=obj_sb[:], in_=obj.rearrange("b i k -> (b i) k"))
+            nc.sync.dma_start(out=obj_rows[:], in_=obj.rearrange("b i k -> (b i) k"))
             load(2)
-            nc.vector.memset(warm[:], 0.0)
-            for plane in (pl_a, pl_b, pl_c):
+            for plane in (rp_plane_low, rp_plane_high, pp_plane):
                 nc.vector.memset(plane[:].bitcast(I32), 0)
             nc.vector.memset(bias_row[:], 0.0)
-            nc.vector.memset(obj_sc[:].rearrange("p g c -> p (g c)").bitcast(I32), 0)
-            nc.scalar.activation(out=warm[:], in_=warm[:], func=ACT.Relu)
+            nc.vector.memset(table_warmer[:], 0.0)
+            nc.scalar.activation(out=table_warmer[:], in_=table_warmer[:], func=ACT.Relu)
             for q in range(4):
                 nc.sync.dma_start(
-                    out=pl_a[32 * q : 32 * q + 16, :].bitcast(I32),
+                    out=rp_plane_low[32 * q : 32 * q + 16, :].bitcast(I32),
                     in_=rp_w_scales[0:4, 4 * q : 4 * q + 4, :].bitcast(I32),
                 )
             for q in range(4):
                 nc.sync.dma_start(
-                    out=pl_b[32 * q : 32 * q + 8, :].bitcast(I32),
+                    out=rp_plane_high[32 * q : 32 * q + 8, :].bitcast(I32),
                     in_=rp_w_scales[4:6, 4 * q : 4 * q + 4, :].bitcast(I32),
                 )
-            nc.sync.dma_start(out=bias_row[0:M_TILES, :], in_=rp_b.rearrange("(m p) -> m p", p=P))
-            nc.sync.dma_start(out=w_obj[0][:].bitcast(I32), in_=rp_words[:, 2:6, 0:512])
-            nc.sync.dma_start(out=w_rel[0][:].bitcast(I32), in_=rp_words[:, 0:2, 0:512])
+            nc.sync.dma_start(out=bias_row[0:M_TILES, :], in_=rp_b.rearrange("(m n) -> m n", n=P))
+            nc.sync.dma_start(out=w_obj[0][:].bitcast(I32), in_=rp_words[:, RECV:6, 0 : NF // 2])
+            nc.sync.dma_start(out=w_rel[0][:].bitcast(I32), in_=rp_words[:, REL:RECV, 0 : NF // 2])
             load(3)
             load(4)
-            nc.sync.dma_start(out=w_obj[1][:].bitcast(I32), in_=rp_words[:, 2:6, 512:1024])
-            nc.sync.dma_start(out=w_rel[1][:].bitcast(I32), in_=rp_words[:, 0:2, 512:1024])
+            nc.sync.dma_start(out=w_obj[1][:].bitcast(I32), in_=rp_words[:, RECV:6, NF // 2 : NF])
+            nc.sync.dma_start(out=w_rel[1][:].bitcast(I32), in_=rp_words[:, REL:RECV, NF // 2 : NF])
             load(5)
+            load(6)
 
             widen(0)
             turn(0, 0)
             turn(0, 1)
-            obj_bank = e_bank()
-            obj_words = obj_sb[:].bitcast(F32)
+            obj_bank = product_bank()
+            obj_words = obj_rows[:].bitcast(F32)
             for g in range(GROUPS):
                 for u in range(2):
                     k = 2 * g + u
@@ -349,115 +358,93 @@ def tile_compositionalkoopmanoperators_pa_w8_kernel(
                     )
             widen(1)
             nc.scalar.copy(
-                out=obj_grp[:].bitcast(F32).rearrange("p (g c u) -> p g c u", g=GROUPS, u=2),
+                out=obj_grouped[:].bitcast(F32).rearrange("p (g c u) -> p g c u", g=GROUPS, u=2),
                 in_=obj_bank[:].rearrange("p (g u c) -> p g c u", g=GROUPS, u=2),
             )
             turn(1, 0)
-            prepare(0, "M")
-            nc.vector.quantize_mx(
-                out=obj_codes[:].rearrange("p g c -> p (g c)").bitcast(FP8X4),
-                scales=obj_sc[:].rearrange("p g c -> p (g c)"),
-                in_=obj_grp[:],
-            )
-            prepare(0, "Q")
-            nc.vector.tensor_copy(out=bias_rowf[:], in_=bias_row[:])
+            scale(0, 0)
+            scale(0, 1)
+            nc.vector.quantize_mx(out=obj_codes[:].bitcast(FP8X4), scales=obj_scales[:], in_=obj_grouped[:])
+            quantise(0, 0)
+            quantise(0, 1)
+            nc.gpsimd.tensor_copy(out=bias_row_f32[:], in_=bias_row[:])
             turn(1, 1)
             widen(2)
-            prepare(1, "M")
+            scale(1, 0)
+            scale(1, 1)
             turn(2, 0)
             turn(2, 1)
-            prepare(1, "Q")
-            bias_bank = e_bank()
-            nc.tensor.transpose(bias_bank[:, 0:P], bias_rowf[:], ident[:])
+            quantise(1, 0)
+            quantise(1, 1)
+            bias_bank = product_bank()
+            nc.tensor.transpose(bias_bank[:, 0:P], bias_row_f32[:], ident[:])
             nc.scalar.copy(out=bias_col[:], in_=bias_bank[:, 0:M_TILES])
             receivers(0)
             senders(0)
             widen(3)
-            for m in range(4):
-                products(0, m, False)
+
+            for tile in slot_tiles(0):
+                multiply(*tile)
             turn(3, 0)
             turn(3, 1)
-            prepare(2, "M")
-            for m in range(4):
-                add_recv(0, m)
-            prepare(2, "Q")
+            scale(2, 0)
+            scale(2, 1)
+            for tile in slot_tiles(0)[: HALF - 1]:
+                add_receiver(*tile)
+            quantise(2, 0)
+            quantise(2, 1)
             widen(4)
-            send_relu(0, 0, False)
-            send_relu(0, 1, False)
+            add_sender_and_relu(0, 0)
+            lift_and_add_receiver(0, HALF - 1)
+            add_sender_and_relu(0, 1)
             receivers(1)
             senders(1)
-            prepare(3, "MQ")
-            send_relu(0, 2, False)
-            send_relu(0, 3, False)
+            scale(3, 0)
+            scale(3, 1)
+            quantise(3, 0)
+            quantise(3, 1)
+            add_sender_and_relu(0, 2)
+            add_sender_and_relu(0, HALF - 1)
             turn(4, 0)
             turn(4, 1)
             widen(5)
-            load(6)
 
             for s in range(1, SLOTS):
-                if s + 6 < SLOTS:
+                if s + 6 < PAIRS:
                     load(s + 6)
                 if s == 1:
                     for q in range(4):
                         nc.sync.dma_start(
-                            out=pl_c[32 * q : 32 * q + 16, :].bitcast(I32),
+                            out=pp_plane[32 * q : 32 * q + 16, :].bitcast(I32),
                             in_=pp_w_scales[:, 4 * q : 4 * q + 4, :].bitcast(I32),
                         )
                 if s in (2, 4, 6, 8):
                     g = s // 2 - 1
                     nc.sync.dma_start(out=w_pp[:, g, :].bitcast(I32), in_=pp_words[:, g, :])
                 if s == 9:
-                    nc.sync.dma_start(out=ppb[:], in_=pp_b.partition_broadcast(P))
+                    nc.sync.dma_start(out=out_bias[:], in_=pp_b.partition_broadcast(P))
                 slot(s)
 
-            out_banks = [e_bank(), e_bank()]
-
-            def out_pass(act_codes, act_scales, g, first, last):
-                for n in range(2):
-                    nc.tensor.matmul_mx(
-                        out=out_banks[n][:],
-                        lhsT=act_codes.bitcast(FP8X4),
-                        lhsT_scale=act_scales,
-                        rhs=w_pp[:, g, 512 * n : 512 * n + 512].bitcast(FP8X4),
-                        rhs_scale=pl_c[4 * g : P, 512 * n : 512 * n + 512],
-                        start=first,
-                        stop=last,
-                    )
-
-            def round_agg(hf):
-                nc.vector.tensor_copy(out=agg_bf[:, hf, :], in_=agg_bank[hf][:])
-
-            def requantise(hf):
-                agg_words = agg_bf[:, hf, :].bitcast(F32)
-                back = x_bank()
-                for u in range(2):
-                    nc.tensor.transpose(back[:, u, 0:P], agg_words[:, u:256:2], ident[:])
-                nc.vector.tensor_copy(
-                    out=agg_grp[:, hf, :].bitcast(F32).rearrange("p (c u) -> p c u", u=2),
-                    in_=back[:, :, 0:P].rearrange("p u c -> p c u"),
-                )
-                nc.vector.quantize_mx(
-                    out=agg_codes[:, hf, :].bitcast(FP8X4), scales=agg_sc[:, hf, :], in_=agg_grp[:, hf, :]
-                )
-
+            out_banks = [product_bank(), product_bank()]
             round_agg(0)
-            for k in [0,1,2]:
-                collect(7, 4 + k)
-            requantise(0)
-            collect(7, 7)
+            for tile in slot_tiles(SLOTS - 1)[: HALF - 1]:
+                collect(*tile)
+            quantise_agg(0)
+            collect(*slot_tiles(SLOTS - 1)[HALF - 1])
             round_agg(1)
             for g in range(GROUPS):
-                out_pass(obj_codes[:, g, :], obj_sc[:, g, :], g, g == 0, False)
-            requantise(1)
-            out_pass(agg_codes[:, 0, :], agg_sc[:, 0, :], 2, False, False)
-            out_pass(agg_codes[:, 1, :], agg_sc[:, 1, :], 3, False, True)
+                cols = slice(P * g, P * g + P)
+                multiply_out(out_banks, obj_codes[:, cols], obj_scales[:, cols], g, g == 0, False)
+            quantise_agg(1)
+            multiply_out(out_banks, agg_codes[:, 0, :], agg_scales[:, 0, :], GROUPS, False, False)
+            multiply_out(out_banks, agg_codes[:, 1, :], agg_scales[:, 1, :], GROUPS + 1, False, True)
             for n in range(4):
-                cols = slice(256 * (n % 2), 256 * (n % 2) + 256)
-                dest = slice(256 * n, 256 * n + 256)
-                res = stream.tile([P, 256], F32, name="res", tag="res", bufs=4)
-                nc.vector.tensor_tensor(out=res[:], in0=out_banks[n // 2][:, cols], in1=ppb[:, dest], op=ALU.add)
+                cols = slice(2 * P * (n % 2), 2 * P * (n % 2) + 2 * P)
+                dest = slice(2 * P * n, 2 * P * n + 2 * P)
+                result = stream.tile([P, 2 * P], F32, name="result", tag="result", bufs=4)
+                nc.vector.tensor_tensor(out=result[:], in0=out_banks[n // 2][:, cols], in1=out_bias[:, dest], op=ALU.add)
                 if n < 3:
-                    nc.scalar.activation(out=res[:], in_=res[:], func=ACT.Relu)
+                    nc.scalar.activation(out=result[:], in_=result[:], func=ACT.Relu)
                 else:
-                    nc.vector.tensor_scalar(out=res[:], in0=res[:], scalar1=0.0, scalar2=None, op0=ALU.max)
-                nc.sync.dma_start(out=out_rows[:, dest], in_=res[:])
+                    nc.vector.tensor_scalar(out=result[:], in0=result[:], scalar1=0.0, scalar2=None, op0=ALU.max)
+                nc.sync.dma_start(out=out_rows[:, dest], in_=result[:])

from contextlib import ExitStack

import concourse.mybir as mybir
from concourse.masks import make_identity

F32 = mybir.dt.float32
BF16 = mybir.dt.bfloat16
I32 = mybir.dt.int32
U32 = mybir.dt.uint32
U8 = mybir.dt.uint8
FP8 = mybir.dt.float8_e4m3fn
FP8X4 = mybir.dt.float8_e4m3fn_x4
ALU = mybir.AluOpType
ACT = mybir.ActivationFunctionType

P = 128
B, N, NF = 4, 32, 1024
T = 4
GROUPS = NF // (P * T)
M_TILES = NF // P
HALF = M_TILES // 2
PAIRS = N // 2
CHUNKS = N // 4
SLOTS = 2 * CHUNKS
COLS = 4 * P
REL, RECV, SEND = 0, 2, 4

FLOPS = 2 * B * N * N * NF * NF + 4 * 2 * B * N * NF * NF


def tile_compositionalkoopmanoperators_pa_w8_kernel(
    tc, rel_enc_bytes, rel_enc_scale, obj, rp_w_words, rp_w_scales, rp_b, pp_w_words, pp_w_scales, pp_b, out
):
    nc = tc.nc
    with ExitStack() as ctx:
        keep = ctx.enter_context(tc.tile_pool(name="keep", bufs=1))
        stream = ctx.enter_context(tc.tile_pool(name="stream", bufs=2))
        psum = ctx.enter_context(tc.psum_pool(name="psum", bufs=1))

        rel_rows = rel_enc_bytes.rearrange("b i j k -> (b i) j k")
        out_rows = out.rearrange("b i n -> (b i) n")
        rp_words = rp_w_words.rearrange("g p n t -> p g (n t)").bitcast(I32)
        pp_words = pp_w_words.rearrange("g p n t -> p g (n t)").bitcast(I32)

        ident = keep.tile([P, P], F32, name="ident")
        make_identity(nc, ident[:])

        rel_scale = keep.tile([P, GROUPS, T], F32, name="rel_scale")
        bias_row = keep.tile([P, P], BF16, name="bias_row")
        bias_row_f32 = keep.tile([P, P], F32, name="bias_row_f32")
        bias_col = keep.tile([P, M_TILES], F32, name="bias_col")
        out_bias = keep.tile([P, NF], BF16, name="out_bias")
        obj_rows = keep.tile([P, NF], BF16, name="obj_rows")
        obj_grouped = keep.tile([P, GROUPS * P * T], BF16, name="obj_grouped", align_bytes=64)
        obj_codes = keep.tile([P, GROUPS * P], U32, name="obj_codes", align_bytes=64)
        obj_scales = keep.tile([P, GROUPS * P], U8, name="obj_scales", align_bytes=64)
        w_rel = [keep.tile([P, 2, NF // 2], U32, name="w_rel%d" % h, align_bytes=64) for h in range(2)]
        w_obj = [keep.tile([P, 4, NF // 2], U32, name="w_obj%d" % h, align_bytes=64) for h in range(2)]
        w_pp = keep.tile([P, 4, NF], U32, name="w_pp", align_bytes=64)
        rp_plane_low = keep.tile([P, NF], U8, name="rp_plane_low", align_bytes=64)
        rp_plane_high = keep.tile([P, NF], U8, name="rp_plane_high", align_bytes=64)
        pp_plane = keep.tile([P, NF], U8, name="pp_plane", align_bytes=64)
        recv = keep.tile([P, M_TILES, P], F32, name="recv")
        send = keep.tile([P, M_TILES, P], F32, name="send")
        agg_rows = keep.tile([P, 2, NF // 2], BF16, name="agg_rows")
        agg_grouped = keep.tile([P, 2, P * T], BF16, name="agg_grouped", align_bytes=64)
        agg_codes = keep.tile([P, 2, P], U32, name="agg_codes", align_bytes=64)
        agg_scales = keep.tile([P, 2, P], U8, name="agg_scales", align_bytes=64)
        table_warmer = keep.tile([P, 1], F32, name="table_warmer")
        turn_token = keep.tile([P, 1], U32, name="turn_token")
        agg_bank = [psum.tile([P, NF // 2], F32, name="agg%d" % h, tag="agg%d" % h, bufs=1) for h in range(2)]

        def product_bank():
            bank = psum.tile([P, COLS], F32, name="product_bank", tag="product_bank", bufs=3)
            return bank

        def turned_bank():
            bank = psum.tile([P, 2, 2 * P], F32, name="turned_bank", tag="turned_bank", bufs=3)
            return bank

        rel_bytes, rel_wide, turned, grouped, codes, scales, products, effects = {}, {}, {}, {}, {}, {}, {}, {}


        def load(p):
            t = stream.tile([P, 2, NF], U8, name="rel_bytes", tag="rel_bytes", bufs=6)
            if p == 0:
                for j in range(2):
                    nc.sync.dma_start(out=t[:, j, :], in_=rel_rows[:, j, :])
            else:
                nc.sync.dma_start(out=t[:], in_=rel_rows[:, 2 * p : 2 * p + 2, :])
            rel_bytes[p] = t

        def widen(p):
            t = stream.tile([P, 2, NF], BF16, name="rel_wide", tag="rel_wide", bufs=3)
            for j in range(2):
                values = rel_bytes[p][:, j, :].bitcast(FP8)
                if p == 0 and j == 1:
                    nc.vector.tensor_copy(out=t[:, j, :], in_=values)
                elif p < 4:
                    nc.scalar.copy(out=t[:, j, :], in_=values)
                else:
                    nc.gpsimd.tensor_copy(out=t[:, j, :], in_=values)
            rel_wide[p] = t

        def turn(p, g):
            words = rel_wide[p][:].bitcast(F32)
            bank = turned_bank()
            for j in range(2):
                for u in range(2):
                    nc.tensor.transpose(
                        bank[:, u, P * j : P * j + P], words[:, j, 256 * g + u : 256 * g + 256 : 2], ident[:]
                    )
            turned[p, g] = bank

        def scale(p, g):
            t = stream.tile([P, 2 * P, T], BF16, name="grouped", tag="grouped", bufs=4, align_bytes=64)
            values = turned[p, g][:].rearrange("p u c -> p (u c)").bitcast(BF16)
            nc.vector.tensor_tensor(
                out=t[:].rearrange("p c (u e) -> p c u e", u=2),
                in0=values.rearrange("p (u c e) -> p c u e", u=2, e=2),
                in1=rel_scale[:, g, :].rearrange("p (o u e) -> p o u e", o=1, u=2).to_broadcast([P, 2 * P, 2, 2]),
                op=ALU.mult,
            )
            grouped[p, g] = t

        def quantise(p, g):
            c, h = p // 2, p % 2
            if c not in codes:
                code_tile = stream.tile([P, GROUPS, COLS], U32, name="codes", tag="codes", bufs=4, align_bytes=64)
                scale_tile = stream.tile([P, GROUPS, COLS], U8, name="scales", tag="scales", bufs=4, align_bytes=64)
                codes[c], scales[c] = code_tile, scale_tile
            cols = slice(2 * P * h, 2 * P * h + 2 * P)
            nc.vector.quantize_mx(
                out=codes[c][:, g, cols].bitcast(FP8X4),
                scales=scales[c][:, g, cols],
                in_=grouped[p, g][:].rearrange("p c t -> p (c t)"),
            )


        def weight(g, m):
            lo = (m % HALF) * P
            if g < RECV:
                words = w_rel[m // HALF][:, g, lo : lo + P]
            else:
                words = w_obj[m // HALF][:, g - RECV, lo : lo + P]
            plane = rp_plane_low if g < SEND else rp_plane_high
            return words.bitcast(FP8X4), plane[4 * (g % 4) : P, m * P : m * P + P]

        def multiply(c, m):
            bank = product_bank()
            for g in range(GROUPS):
                w, w_scale = weight(REL + g, m)
                nc.tensor.matmul_mx(
                    out=bank[:],
                    lhsT=w,
                    lhsT_scale=w_scale,
                    rhs=codes[c][:, g, :].bitcast(FP8X4),
                    rhs_scale=scales[c][:, g, :],
                    start=(g == 0),
                    stop=(g == GROUPS - 1),
                )
            products[c, m] = bank

        def effect_tile():
            t = stream.tile([P, 4, P], F32, name="effect", tag="effect", bufs=14)
            return t

        def recv_columns(m):
            return recv[:, m : m + 1, :].to_broadcast([P, 4, P])

        def add_receiver(c, m):
            t = effect_tile()
            nc.vector.tensor_tensor(
                out=t[:], in0=products[c, m][:].rearrange("p (j r) -> p j r", j=4), in1=recv_columns(m), op=ALU.add
            )
            effects[c, m] = t

        def lift_and_add_receiver(c, m):
            t = effect_tile()
            nc.scalar.copy(out=t[:].rearrange("p j r -> p (j r)"), in_=products[c, m][:])
            nc.gpsimd.tensor_tensor(out=t[:], in0=t[:], in1=recv_columns(m), op=ALU.add)
            effects[c, m] = t

        def add_sender_and_relu(c, m):
            t = effects[c, m]
            for j in range(4):
                for b in range(B):
                    sender = N * b + 4 * c + j
                    nc.scalar.activation(
                        out=t[:, j, N * b : N * b + N],
                        in_=t[:, j, N * b : N * b + N],
                        func=ACT.Relu,
                        bias=send[:, m, sender : sender + 1],
                    )

        def add_sender(c, m):
            t = effects[c, m][:].rearrange("p j (b i) -> p j b i", b=B)
            terms = send[:, m, :].rearrange("p (b j o) -> p j b o", b=B, o=1)[:, 4 * c : 4 * c + 4]
            nc.vector.tensor_tensor(out=t, in0=t, in1=terms.to_broadcast([P, 4, B, N]), op=ALU.add)

        def relu(c, m):
            t = effects[c, m]
            nc.scalar.activation(out=t[:], in_=t[:], func=ACT.Relu)

        def collect(c, m):
            k = m % HALF
            for j in range(4):
                nc.tensor.matmul(
                    agg_bank[m // HALF][:, P * k : P * k + P],
                    lhsT=effects[c, m][:, j, :],
                    rhs=ident[:],
                    is_transpose=True,
                    start=(c == 0 and k == 0 and j == 0),
                    stop=(c == CHUNKS - 1 and k == HALF - 1 and j == 3),
                )

        def multiply_objects(group, h):
            bank = product_bank()
            for k in range(HALF):
                for g in range(GROUPS):
                    w, w_scale = weight(group + g, HALF * h + k)
                    nc.tensor.matmul_mx(
                        out=bank[:, P * k : P * k + P],
                        lhsT=w,
                        lhsT_scale=w_scale,
                        rhs=obj_codes[:, P * g : P * g + P].bitcast(FP8X4),
                        rhs_scale=obj_scales[:, P * g : P * g + P],
                        start=(g == 0),
                        stop=(g == GROUPS - 1),
                    )
            return bank

        def receivers(h):
            bank = multiply_objects(RECV, h)
            nc.scalar.copy(out=recv[:, HALF * h : HALF * h + HALF, :].rearrange("p m c -> p (m c)"), in_=bank[:])

        def senders(h):
            bank = multiply_objects(SEND, h)
            for k in range(HALF):
                m = HALF * h + k
                nc.scalar.activation(
                    out=send[:, m, :], in_=bank[:, P * k : P * k + P], func=ACT.Identity, bias=bias_col[:, m : m + 1]
                )

        def slot_tiles(s):
            return [(s // 2, HALF * (s % 2) + k) for k in range(HALF)]

        def slot(s):
            tiles = slot_tiles(s)
            preparing = s + 3 < PAIRS
            lifted = tiles[HALF - 1]
            for tile in tiles:
                multiply(*tile)
            for tile in tiles:
                if tile != lifted or not preparing:
                    add_receiver(*tile)
            if preparing:
                scale(s + 3, 0)
                scale(s + 3, 1)
                quantise(s + 3, 0)
                quantise(s + 3, 1)
            else:
                add_sender(*lifted)
            for tile in slot_tiles(s - 1):
                collect(*tile)
            if s + 4 < PAIRS:
                turn(s + 4, 0)
                turn(s + 4, 1)
            add_sender_and_relu(*tiles[0])
            if preparing:
                lift_and_add_receiver(*lifted)
            add_sender_and_relu(*tiles[1])
            add_sender_and_relu(*tiles[2])
            if preparing:
                add_sender_and_relu(*lifted)
            else:
                relu(*lifted)
            if s + 5 < PAIRS:
                c, h = (s + 3) // 2, (s + 3) % 2
                nc.gpsimd.tensor_copy(
                    out=turn_token[:].bitcast(I32), in_=codes[c][:, 0, 2 * P * h : 2 * P * h + 1].bitcast(I32)
                )
                widen(s + 5)


        def multiply_out(banks, act_codes, act_scales, g, first, last):
            for n in range(2):
                cols = slice(COLS * n, COLS * n + COLS)
                nc.tensor.matmul_mx(
                    out=banks[n][:],
                    lhsT=act_codes.bitcast(FP8X4),
                    lhsT_scale=act_scales,
                    rhs=w_pp[:, g, cols].bitcast(FP8X4),
                    rhs_scale=pp_plane[4 * g : P, cols],
                    start=first,
                    stop=last,
                )

        def round_agg(h):
            nc.vector.tensor_copy(out=agg_rows[:, h, :], in_=agg_bank[h][:])

        def quantise_agg(h):
            words = agg_rows[:, h, :].bitcast(F32)
            bank = turned_bank()
            for u in range(2):
                nc.tensor.transpose(bank[:, u, 0:P], words[:, u : 2 * P : 2], ident[:])
            nc.vector.tensor_copy(
                out=agg_grouped[:, h, :].bitcast(F32).rearrange("p (c u) -> p c u", u=2),
                in_=bank[:, :, 0:P].rearrange("p u c -> p c u"),
            )
            nc.vector.quantize_mx(
                out=agg_codes[:, h, :].bitcast(FP8X4), scales=agg_scales[:, h, :], in_=agg_grouped[:, h, :]
            )

        with tc.manual_schedule():
            load(0)
            nc.sync.dma_start(
                out=rel_scale[:], in_=rel_enc_scale.rearrange("a b c (g p t) -> p (a b c g) t", p=P, t=T)
            )
            load(1)
            nc.sync.dma_start(out=obj_rows[:], in_=obj.rearrange("b i k -> (b i) k"))
            load(2)
            for plane in (rp_plane_low, rp_plane_high, pp_plane):
                nc.vector.memset(plane[:].bitcast(I32), 0)
            nc.vector.memset(bias_row[:], 0.0)
            nc.vector.memset(table_warmer[:], 0.0)
            nc.scalar.activation(out=table_warmer[:], in_=table_warmer[:], func=ACT.Relu)
            for q in range(4):
                nc.sync.dma_start(
                    out=rp_plane_low[32 * q : 32 * q + 16, :].bitcast(I32),
                    in_=rp_w_scales[0:4, 4 * q : 4 * q + 4, :].bitcast(I32),
                )
            for q in range(4):
                nc.sync.dma_start(
                    out=rp_plane_high[32 * q : 32 * q + 8, :].bitcast(I32),
                    in_=rp_w_scales[4:6, 4 * q : 4 * q + 4, :].bitcast(I32),
                )
            nc.sync.dma_start(out=bias_row[0:M_TILES, :], in_=rp_b.rearrange("(m n) -> m n", n=P))
            nc.sync.dma_start(out=w_obj[0][:].bitcast(I32), in_=rp_words[:, RECV:6, 0 : NF // 2])
            nc.sync.dma_start(out=w_rel[0][:].bitcast(I32), in_=rp_words[:, REL:RECV, 0 : NF // 2])
            load(3)
            load(4)
            nc.sync.dma_start(out=w_obj[1][:].bitcast(I32), in_=rp_words[:, RECV:6, NF // 2 : NF])
            nc.sync.dma_start(out=w_rel[1][:].bitcast(I32), in_=rp_words[:, REL:RECV, NF // 2 : NF])
            load(5)
            load(6)

            widen(0)
            turn(0, 0)
            turn(0, 1)
            obj_bank = product_bank()
            obj_words = obj_rows[:].bitcast(F32)
            for g in range(GROUPS):
                for u in range(2):
                    k = 2 * g + u
                    nc.tensor.transpose(
                        obj_bank[:, P * k : P * k + P], obj_words[:, 256 * g + u : 256 * g + 256 : 2], ident[:]
                    )
            widen(1)
            nc.scalar.copy(
                out=obj_grouped[:].bitcast(F32).rearrange("p (g c u) -> p g c u", g=GROUPS, u=2),
                in_=obj_bank[:].rearrange("p (g u c) -> p g c u", g=GROUPS, u=2),
            )
            turn(1, 0)
            scale(0, 0)
            scale(0, 1)
            nc.vector.quantize_mx(out=obj_codes[:].bitcast(FP8X4), scales=obj_scales[:], in_=obj_grouped[:])
            quantise(0, 0)
            quantise(0, 1)
            nc.gpsimd.tensor_copy(out=bias_row_f32[:], in_=bias_row[:])
            turn(1, 1)
            widen(2)
            scale(1, 0)
            scale(1, 1)
            turn(2, 0)
            turn(2, 1)
            quantise(1, 0)
            quantise(1, 1)
            bias_bank = product_bank()
            nc.tensor.transpose(bias_bank[:, 0:P], bias_row_f32[:], ident[:])
            nc.scalar.copy(out=bias_col[:], in_=bias_bank[:, 0:M_TILES])
            receivers(0)
            senders(0)
            widen(3)

            for tile in slot_tiles(0):
                multiply(*tile)
            turn(3, 0)
            turn(3, 1)
            scale(2, 0)
            scale(2, 1)
            for tile in slot_tiles(0)[: HALF - 1]:
                add_receiver(*tile)
            quantise(2, 0)
            quantise(2, 1)
            widen(4)
            add_sender_and_relu(0, 0)
            lift_and_add_receiver(0, HALF - 1)
            add_sender_and_relu(0, 1)
            receivers(1)
            senders(1)
            scale(3, 0)
            scale(3, 1)
            quantise(3, 0)
            quantise(3, 1)
            add_sender_and_relu(0, 2)
            add_sender_and_relu(0, HALF - 1)
            turn(4, 0)
            turn(4, 1)
            widen(5)

            for s in range(1, SLOTS):
                if s + 6 < PAIRS:
                    load(s + 6)
                if s == 1:
                    for q in range(4):
                        nc.sync.dma_start(
                            out=pp_plane[32 * q : 32 * q + 16, :].bitcast(I32),
                            in_=pp_w_scales[:, 4 * q : 4 * q + 4, :].bitcast(I32),
                        )
                if s in (2, 4, 6, 8):
                    g = s // 2 - 1
                    nc.sync.dma_start(out=w_pp[:, g, :].bitcast(I32), in_=pp_words[:, g, :])
                if s == 9:
                    nc.sync.dma_start(out=out_bias[:], in_=pp_b.partition_broadcast(P))
                slot(s)

            out_banks = [product_bank(), product_bank()]
            round_agg(0)
            for tile in slot_tiles(SLOTS - 1)[: HALF - 1]:
                collect(*tile)
            quantise_agg(0)
            collect(*slot_tiles(SLOTS - 1)[HALF - 1])
            round_agg(1)
            for g in range(GROUPS):
                cols = slice(P * g, P * g + P)
                multiply_out(out_banks, obj_codes[:, cols], obj_scales[:, cols], g, g == 0, False)
            quantise_agg(1)
            multiply_out(out_banks, agg_codes[:, 0, :], agg_scales[:, 0, :], GROUPS, False, False)
            multiply_out(out_banks, agg_codes[:, 1, :], agg_scales[:, 1, :], GROUPS + 1, False, True)
            for n in range(4):
                cols = slice(2 * P * (n % 2), 2 * P * (n % 2) + 2 * P)
                dest = slice(2 * P * n, 2 * P * n + 2 * P)
                result = stream.tile([P, 2 * P], F32, name="result", tag="result", bufs=4)
                nc.vector.tensor_tensor(out=result[:], in0=out_banks[n // 2][:, cols], in1=out_bias[:, dest], op=ALU.add)
                if n < 3:
                    nc.scalar.activation(out=result[:], in_=result[:], func=ACT.Relu)
                else:
                    nc.vector.tensor_scalar(out=result[:], in0=result[:], scalar1=0.0, scalar2=None, op0=ALU.max)
                nc.sync.dma_start(out=out_rows[:, dest], in_=result[:])
